import numpy as np
import ml_dtypes


def mxq(x, axis, fmt="e4m3"):
    dtype, down = {"e4m3": (ml_dtypes.float8_e4m3fn, 7), "e5m2": (ml_dtypes.float8_e5m2, 14)}[fmt]
    v = np.moveaxis(np.asarray(x, np.float32).astype(ml_dtypes.bfloat16).astype(np.float64), axis, -1)
    blocks = v.reshape(v.shape[:-1] + (-1, 32))
    amax = np.abs(blocks).max(-1, keepdims=True)
    byte = np.maximum(np.where(amax > 0, np.frexp(amax)[1] - 1 + 127, 0) - down, 1)
    scale = np.exp2(byte - 127.0)
    codes = (blocks / scale).astype(np.float32).astype(dtype).astype(np.float64)
    return np.moveaxis((codes * scale).reshape(v.shape), -1, axis)


WIDE = False


def mx_kscale(k):
    if not WIDE:
        return np.ones(k)
    levels = np.array([10, -10, 5, -5, 0])
    a = np.random.permutation(np.resize(levels, k // 512 * 4)).reshape(k // 512, 4)
    idx = np.arange(k)
    return np.exp2(a[idx // 512, idx % 128 // 32])


BF16 = ml_dtypes.bfloat16


def bf(x):
    return np.asarray(x, np.float32).astype(BF16)


def f64(x):
    return np.asarray(x).astype(np.float64)


B, N, DIN, DS, GE, HID, NS, KC = 8, 512, 64, 64, 8, 32, 2, 3
DO = DS
C = DIN + DS + DS
F = NS * KC * C
SHARP = 4.0


def sigmoid(v):
    return 1.0 / (1.0 + np.exp(-v))


def softmax(v):
    e = np.exp(v - v.max(-1, keepdims=True))
    return e / e.sum(-1, keepdims=True)


def setup_inputs():
    s = mx_kscale(N)
    adj = softmax(SHARP * np.random.standard_normal((NS, B, N, N)))
    return {"xg_gate": bf(np.random.standard_normal((B, N, F)) * 0.8),
            "gate_w_z": bf(np.random.standard_normal((F, DO + DO)) * 1.5 / np.sqrt(F)),
            "gate_b_z": bf(np.random.standard_normal(DO + DO) * 0.5),
            "xt": bf(np.random.standard_normal((B, N, DIN)) / s[:, None]),
            "state1": bf(np.random.standard_normal((B, N, DS)) / s[:, None]),
            "state2": bf(np.random.standard_normal((B, N, DS)) / s[:, None]),
            "supports": bf(adj * s / s[:, None])}


def reference(xg_gate, gate_w_z, gate_b_z, xt, state1, state2, supports):
    z = sigmoid(f64(xg_gate) @ f64(gate_w_z) + f64(gate_b_z))
    cand = np.concatenate([f64(xt), z[..., :DO] * f64(state1), z[..., DO:] * f64(state2)], axis=-1)
    cq = mxq(cand, 1, "e4m3")
    terms = []
    for i in range(NS):
        aq = mxq(f64(supports)[i], 2, "e4m3")
        t_prev, t_cur = cand, aq @ cq
        ts = [t_prev, t_cur]
        for _ in range(KC - len(ts)):
            t_prev, t_cur = t_cur, 2.0 * (aq @ mxq(t_cur, 1, "e4m3")) - t_prev
            ts.append(t_cur)
        terms.extend(ts)
    return np.concatenate(terms, axis=-1)

@@ -1,0 +1,280 @@
+from contextlib import ExitStack
+
+import concourse.mybir as mybir
+from concourse.masks import make_identity
+
+F32 = mybir.dt.float32
+BF16 = mybir.dt.bfloat16
+U32 = mybir.dt.uint32
+U8 = mybir.dt.uint8
+FP8X4 = mybir.dt.float8_e4m3fn_x4
+ALU = mybir.AluOpType
+ACT = mybir.ActivationFunctionType
+
+P = 128
+B, NODES, F, D, C = 8, 512, 1152, 64, 192
+G = 2 * D
+NS = 2
+T = 4
+CP = 256
+FW = F // 2
+NCH = 4
+FLOPS = 2 * B * NODES * F * G + 2 * NS * 2 * B * NODES * NODES * C
+MANUAL = True
+LAYOUT = "upe"
+
+
+def tile_dgggl_pa_t_kernel(tc, xg_gate, gate_w_z, gate_b_z, xt, state1, state2, supports, out):
+    nc = tc.nc
+    with ExitStack() as ctx:
+        const = ctx.enter_context(tc.tile_pool(name="const", bufs=1))
+        loads = ctx.enter_context(tc.tile_pool(name="loads", bufs=3))
+        work = ctx.enter_context(tc.tile_pool(name="work", bufs=2))
+        stages = ctx.enter_context(tc.tile_pool(name="stages", bufs=3))
+        psum = ctx.enter_context(tc.psum_pool(name="psum", bufs=1))
+        if MANUAL:
+            ctx.enter_context(tc.manual_schedule())
+
+        def nodes_view(ap):
+            if LAYOUT == "upe":
+                return ap.rearrange("(u p e) f -> p u (e f)", u=2, e=2)
+            return ap.rearrange("(p u e) f -> p u (e f)", u=2, e=2)
+
+        ident_f = const.tile([P, P], F32, name="ident_f")
+        make_identity(nc, ident_f[:])
+        ident_b = const.tile([P, P], BF16, name="ident_b")
+        make_identity(nc, ident_b[:])
+        w_sb = const.tile([P, NCH, 2, G], BF16, name="w_sb")
+        wt_sb = const.tile([P, G], BF16, name="wt_sb")
+        bias_b = const.tile([P, 1], BF16, name="bias_b")
+        bias_f = const.tile([P, 1], F32, name="bias_f")
+        xt_sb = const.tile([P, B, T, D], BF16, name="xt_sb")
+        st_sb = const.tile([P, B, 2, T, D], BF16, name="st_sb")
+        cg = [const.tile([P, CP, T], BF16, name="cg%d" % k, align_bytes=64) for k in range(2)]
+        tg = [const.tile([P, CP, T], BF16, name="tg%d" % k, align_bytes=64) for k in range(4)]
+        for g in cg + tg:
+            nc.vector.memset(g[:, C:CP, :], 0.0)
+
+        xg_t, a_t, xT_t, xTt_t, zT_t, stage_t, zps_t = {}, {}, {}, {}, {}, {}, {}
+        cc_t, cs_t, ac_t, as_t, tc_t, ts_t, aps_t, ag_t, xps_t = {}, {}, {}, {}, {}, {}, {}, {}, {}
+        cnt = {"T": 0, "X": 0}
+
+        def bank(kind, n, dtype=F32, shape=None):
+            k = cnt[kind] % n
+            cnt[kind] += 1
+            return psum.tile(shape or [P, 512], dtype, name="%s%d" % (kind, k), tag="%s%d" % (kind, k))
+
+        def load_x(b):
+            xg_sb = loads.tile([P, T * F], BF16, name="xg_sb")
+            xg_t[b] = xg_sb
+            nc.sync.dma_start(out=xg_sb[:].rearrange("p (u x) -> p u x", u=2), in_=nodes_view(xg_gate[b]))
+
+        def load_a(b):
+            a_sb = loads.tile([P, NS, T * NODES], BF16, name="a_sb")
+            a_t[b] = a_sb
+            for i in range(NS):
+                nc.sync.dma_start(out=a_sb[:, i, :].rearrange("p (u x) -> p u x", u=2), in_=nodes_view(supports[i, b]))
+
+        def load_consts():
+            nc.sync.dma_start(out=w_sb[:].rearrange("p c e g -> p c (e g)"),
+                              in_=gate_w_z[0:NCH * 2 * P, :].rearrange("(c w e) g -> w c (e g)", c=NCH, e=2))
+            nc.sync.dma_start(out=wt_sb[:], in_=gate_w_z[NCH * 2 * P:F, :])
+            with nc.allow_non_contiguous_dma(reason="one bias value to a partition"):
+                nc.sync.dma_start(out=bias_b[:], in_=gate_b_z.rearrange("(g o) -> g o", o=1))
+            nc.vector.tensor_copy(out=bias_f[:], in_=bias_b[:])
+
+        def load_states(b0, b1):
+            srcs = ((xt, xt_sb[:, b0:b1]), (state1, st_sb[:, b0:b1, 0]), (state2, st_sb[:, b0:b1, 1]))
+            if LAYOUT == "upe":
+                for u in range(2):
+                    for src, dst in srcs:
+                        nc.sync.dma_start(out=dst[:, :, 2 * u:2 * u + 2, :].rearrange("p b e d -> p b (e d)"),
+                                          in_=src[b0:b1].rearrange("b (u p e) d -> u p b (e d)", u=2, e=2)[u])
+            else:
+                for src, dst in srcs:
+                    nc.sync.dma_start(out=dst.rearrange("p b t d -> p b (t d)"),
+                                      in_=src[b0:b1].rearrange("b (p t) d -> p b (t d)", t=T))
+
+        def t1(b, chunks):
+            if b not in xT_t:
+                xT_t[b] = work.tile([P, NCH * NODES], F32, name="xT_sb")
+                xTt_t[b] = work.tile([P, NODES], BF16, name="xTt_sb")
+            xw = xg_t[b][:].bitcast(F32)
+            for c in chunks:
+                if c < NCH:
+                    ps = bank("T", 4)
+                    for t in range(T):
+                        nc.tensor.transpose(ps[:, P * t:P * t + P], xw[:, FW * t + P * c:FW * t + P * c + P], ident_f[:])
+                    nc.scalar.copy(out=xT_t[b][:, NODES * c:NODES * c + NODES], in_=ps[:])
+                else:
+                    ps = bank("T", 4, BF16)
+                    for t in range(T):
+                        nc.tensor.transpose(ps[:, P * t:P * t + P], xg_t[b][:, F * t + 2 * P * NCH:F * t + F], ident_b[:])
+                    nc.scalar.copy(out=xTt_t[b][:], in_=ps[:])
+
+        def gate(b):
+            ps = psum.tile([P, NODES], F32, name="G", tag="G")
+            xb = xT_t[b][:].bitcast(BF16).rearrange("p (c n e) -> p c n e", c=NCH, e=2)
+            for c in range(NCH):
+                for e in range(2):
+                    nc.tensor.matmul(out=ps[:], lhsT=w_sb[:, c, e, :], rhs=xb[:, c, :, e], start=(c == 0 and e == 0), stop=False)
+            nc.tensor.matmul(out=ps[:], lhsT=wt_sb[:], rhs=xTt_t[b][:], start=False, stop=True)
+            zT_t[b] = work.tile([P, NODES], F32, name="zT_sb")
+            nc.scalar.activation(out=zT_t[b][:], in_=ps[:], func=ACT.Sigmoid, bias=bias_f[:, 0:1], scale=1.0)
+
+        def cgx(b):
+            nc.vector.tensor_copy(out=cg[b % 2][:, 0:D, :], in_=xt_sb[:, b].rearrange("p t c -> p c t"))
+
+        def zb_pe(b):
+            ps = bank("T", 4)
+            zps_t[b] = ps
+            for t in range(T):
+                nc.tensor.transpose(ps[:, P * t:P * t + P], zT_t[b][:, P * t:P * t + P], ident_f[:])
+
+        def cand(b):
+            stage = stages.tile([P, T, F], F32, name="stage")
+            stage_t[b] = stage
+            nc.vector.tensor_tensor(out=stage[:, :, D:C].rearrange("p t (s d) -> p t s d", s=2),
+                                    in0=zps_t[b][:].rearrange("p (t s d) -> p t s d", t=T, s=2),
+                                    in1=st_sb[:, b].rearrange("p s t d -> p t s d"), op=ALU.mult)
+            g = cg[b % 2]
+            nc.vector.tensor_copy(out=g[:, D:C, :], in_=stage[:, :, D:C].rearrange("p t c -> p c t"))
+            nc.vector.tensor_copy(out=stage[:, :, 0:D], in_=xt_sb[:, b])
+            cc_t[b] = work.tile([P, CP], U32, name="c_codes", align_bytes=64)
+            cs_t[b] = work.tile([P, CP], U8, name="c_scales", align_bytes=64)
+            nc.vector.quantize_mx(out=cc_t[b][:].bitcast(FP8X4), scales=cs_t[b][:], in_=g[:].rearrange("p c t -> p (c t)"))
+
+        def dup(b):
+            nc.vector.tensor_copy(out=stage_t[b][:, :, 3 * C:4 * C], in_=stage_t[b][:, :, 0:C])
+
+        def ta_pe(b, i):
+            aw = a_t[b][:, i, :].bitcast(F32).rearrange("p (j w) -> p j w", j=T)
+            for h in range(2):
+                ps = bank("T", 4)
+                aps_t[(b, i, h)] = ps
+                for u in range(2):
+                    for jj in range(2):
+                        j = 2 * h + jj
+                        if LAYOUT == "upe":
+                            src = aw[:, j, P * u:P * u + P]
+                        else:
+                            src = aw[:, j, :].rearrange("p (w u) -> p u w", u=2)[:, u, :]
+                        nc.tensor.transpose(ps[:, 256 * u + P * jj:256 * u + P * jj + P], src, ident_f[:])
+
+        def ta_exit(b, i, engines):
+            ag = work.tile([P, NODES * 2], F32, name="ag", bufs=3, align_bytes=64)
+            ag_t[(b, i)] = ag
+            for h in range(2):
+                src = aps_t[(b, i, h)][:].rearrange("p (u n) -> p n u", u=2)
+                dst = ag[:, 512 * h:512 * h + 512].rearrange("p (n u) -> p n u", u=2)
+                if engines[h] == "s":
+                    nc.scalar.copy(out=dst, in_=src)
+                else:
+                    nc.vector.tensor_copy(out=dst, in_=src)
+
+        def ta_quant(b, i):
+            ac_t[(b, i)] = work.tile([P, NODES], U32, name="a_codes", bufs=4, align_bytes=64)
+            as_t[(b, i)] = work.tile([P, NODES], U8, name="a_scales", bufs=4, align_bytes=64)
+            nc.vector.quantize_mx(out=ac_t[(b, i)][:].bitcast(FP8X4), scales=as_t[(b, i)][:], in_=ag_t[(b, i)][:].bitcast(BF16))
+
+        def mx(b, i, h, codes, scales):
+            ps = bank("X", 3, F32, [P, 2, CP])
+            for jj in range(2):
+                j = 2 * h + jj
+                nc.tensor.matmul_mx(out=ps[:, jj, :], lhsT=ac_t[(b, i)][:, P * j:P * j + P].bitcast(FP8X4),
+                                    lhsT_scale=as_t[(b, i)][:, P * j:P * j + P],
+                                    rhs=codes[:].bitcast(FP8X4), rhs_scale=scales[:], start=True, stop=True)
+            return ps
+
+        def x1(b, i):
+            o = 3 * C * i + C
+            for h in range(2):
+                ps = mx(b, i, h, cc_t[b], cs_t[b])
+                nc.scalar.copy(out=stage_t[b][:, 2 * h:2 * h + 2, o:o + C], in_=ps[:, :, 0:C])
+
+        def x1_group(b, i):
+            o = 3 * C * i + C
+            nc.vector.tensor_copy(out=tg[(2 * b + i) % 4][:, 0:C, :], in_=stage_t[b][:, :, o:o + C].rearrange("p t c -> p c t"))
+
+        def x1_quant(b, i):
+            g = tg[(2 * b + i) % 4]
+            tc_t[(b, i)] = work.tile([P, CP], U32, name="t_codes", bufs=4, align_bytes=64)
+            ts_t[(b, i)] = work.tile([P, CP], U8, name="t_scales", bufs=4, align_bytes=64)
+            nc.vector.quantize_mx(out=tc_t[(b, i)][:].bitcast(FP8X4), scales=ts_t[(b, i)][:], in_=g[:].rearrange("p c t -> p (c t)"))
+
+        def x2_pe(b, i, h):
+            xps_t[(b, i, h)] = mx(b, i, h, tc_t[(b, i)], ts_t[(b, i)])
+
+        def x2_exit(b, i, h):
+            o = 3 * C * i + 2 * C
+            nc.vector.scalar_tensor_tensor(out=stage_t[b][:, 2 * h:2 * h + 2, o:o + C], in0=xps_t[(b, i, h)][:, :, 0:C], scalar=2.0,
+                                           in1=stage_t[b][:, 2 * h:2 * h + 2, 0:C], op0=ALU.mult, op1=ALU.subtract)
+
+        def store(b, u):
+            nc.sync.dma_start(out=nodes_view(out[b])[:, u, :], in_=stage_t[b][:, 2 * u:2 * u + 2, :].rearrange("p e f -> p (e f)"))
+
+        def late(b):
+            x2_exit(b, 0, 1)
+            x2_exit(b, 1, 1)
+            store(b, 1)
+
+        load_x(0)
+        load_consts()
+        load_a(0)
+        load_x(1)
+        load_states(0, 2)
+        load_a(1)
+        load_states(2, B)
+        load_x(2)
+        load_a(2)
+        cgx(0)
+        for pi in range(-2, B - 1):
+            b2, b1 = pi + 2, pi + 1
+            go2, go1 = b2 < B, b1 >= 0
+            if pi >= -1 and pi + 4 < B:
+                load_x(pi + 4)
+                load_a(pi + 4)
+            if go2:
+                t1(b2, [0, 1])
+            if go1:
+                zb_pe(b1)
+                cand(b1)
+            if b1 >= 1:
+                late(b1 - 1)
+            if go2:
+                t1(b2, [2, 3, 4])
+                if pi == -2:
+                    gate(b2)
+                ta_pe(b2, 0)
+                ta_pe(b2, 1)
+            if go1:
+                if b1 + 1 < B:
+                    cgx(b1 + 1)
+            if go2:
+                ta_exit(b2, 0, "ss")
+            if go1:
+                x1(b1, 0)
+                x1(b1, 1)
+                x1_group(b1, 0)
+            if go2:
+                ta_quant(b2, 0)
+            if go1:
+                x1_quant(b1, 0)
+                x1_group(b1, 1)
+                dup(b1)
+                x1_quant(b1, 1)
+            if go2:
+                ta_exit(b2, 1, "ss")
+                if pi > -2:
+                    gate(b2)
+            if go1:
+                x2_pe(b1, 0, 0)
+                x2_pe(b1, 1, 0)
+                x2_exit(b1, 0, 0)
+                x2_exit(b1, 1, 0)
+                store(b1, 0)
+                x2_pe(b1, 0, 1)
+                x2_pe(b1, 1, 1)
+            if go2:
+                ta_quant(b2, 1)
+        late(B - 1)

@@ -21,7 +21,7 @@ FW = F // 2
 NCH = 4
 FLOPS = 2 * B * NODES * F * G + 2 * NS * 2 * B * NODES * NODES * C
 MANUAL = True
-LAYOUT = "upe"
+LAYOUT = "pt"
 
 
 def tile_dgggl_pa_t_kernel(tc, xg_gate, gate_w_z, gate_b_z, xt, state1, state2, supports, out):

@@ -21,7 +21,8 @@ FW = F // 2
 NCH = 4
 FLOPS = 2 * B * NODES * F * G + 2 * NS * 2 * B * NODES * NODES * C
 MANUAL = True
-LAYOUT = "pt"
+LAYOUT = "upe"
+NROT = 7
 
 
 def tile_dgggl_pa_t_kernel(tc, xg_gate, gate_w_z, gate_b_z, xt, state1, state2, supports, out):
@@ -30,7 +31,7 @@ def tile_dgggl_pa_t_kernel(tc, xg_gate, gate_w_z, gate_b_z, xt, state1, state2, 
         const = ctx.enter_context(tc.tile_pool(name="const", bufs=1))
         loads = ctx.enter_context(tc.tile_pool(name="loads", bufs=3))
         work = ctx.enter_context(tc.tile_pool(name="work", bufs=2))
-        stages = ctx.enter_context(tc.tile_pool(name="stages", bufs=3))
+        stages = ctx.enter_context(tc.tile_pool(name="stages", bufs=4))
         psum = ctx.enter_context(tc.psum_pool(name="psum", bufs=1))
         if MANUAL:
             ctx.enter_context(tc.manual_schedule())
@@ -55,14 +56,14 @@ def tile_dgggl_pa_t_kernel(tc, xg_gate, gate_w_z, gate_b_z, xt, state1, state2, 
         for g in cg + tg:
             nc.vector.memset(g[:, C:CP, :], 0.0)
 
-        xg_t, a_t, xT_t, xTt_t, zT_t, stage_t, zps_t = {}, {}, {}, {}, {}, {}, {}
+        xg_t, a_t, xT_t, xTt_t, zT_t, stage_t, zps_t, gps_t = {}, {}, {}, {}, {}, {}, {}, {}
         cc_t, cs_t, ac_t, as_t, tc_t, ts_t, aps_t, ag_t, xps_t = {}, {}, {}, {}, {}, {}, {}, {}, {}
-        cnt = {"T": 0, "X": 0}
+        cnt = {"R": 0}
 
-        def bank(kind, n, dtype=F32, shape=None):
-            k = cnt[kind] % n
-            cnt[kind] += 1
-            return psum.tile(shape or [P, 512], dtype, name="%s%d" % (kind, k), tag="%s%d" % (kind, k))
+        def bank(dtype=F32, shape=None):
+            k = cnt["R"] % NROT
+            cnt["R"] += 1
+            return psum.tile(shape or [P, 512], dtype, name="R%d" % k, tag="R%d" % k)
 
         def load_x(b):
             xg_sb = loads.tile([P, T * F], BF16, name="xg_sb")
@@ -95,38 +96,38 @@ def tile_dgggl_pa_t_kernel(tc, xg_gate, gate_w_z, gate_b_z, xt, state1, state2, 
                     nc.sync.dma_start(out=dst.rearrange("p b t d -> p b (t d)"),
                                       in_=src[b0:b1].rearrange("b (p t) d -> p b (t d)", t=T))
 
-        def t1(b, chunks):
+        def t1(b, c):
             if b not in xT_t:
                 xT_t[b] = work.tile([P, NCH * NODES], F32, name="xT_sb")
                 xTt_t[b] = work.tile([P, NODES], BF16, name="xTt_sb")
             xw = xg_t[b][:].bitcast(F32)
-            for c in chunks:
-                if c < NCH:
-                    ps = bank("T", 4)
-                    for t in range(T):
-                        nc.tensor.transpose(ps[:, P * t:P * t + P], xw[:, FW * t + P * c:FW * t + P * c + P], ident_f[:])
-                    nc.scalar.copy(out=xT_t[b][:, NODES * c:NODES * c + NODES], in_=ps[:])
-                else:
-                    ps = bank("T", 4, BF16)
-                    for t in range(T):
-                        nc.tensor.transpose(ps[:, P * t:P * t + P], xg_t[b][:, F * t + 2 * P * NCH:F * t + F], ident_b[:])
-                    nc.scalar.copy(out=xTt_t[b][:], in_=ps[:])
+            if c < NCH:
+                ps = bank()
+                for t in range(T):
+                    nc.tensor.transpose(ps[:, P * t:P * t + P], xw[:, FW * t + P * c:FW * t + P * c + P], ident_f[:])
+                nc.scalar.copy(out=xT_t[b][:, NODES * c:NODES * c + NODES], in_=ps[:])
+            else:
+                ps = bank(BF16)
+                for t in range(T):
+                    nc.tensor.transpose(ps[:, P * t:P * t + P], xg_t[b][:, F * t + 2 * P * NCH:F * t + F], ident_b[:])
+                nc.scalar.copy(out=xTt_t[b][:], in_=ps[:])
 
-        def gate(b):
-            ps = psum.tile([P, NODES], F32, name="G", tag="G")
-            xb = xT_t[b][:].bitcast(BF16).rearrange("p (c n e) -> p c n e", c=NCH, e=2)
-            for c in range(NCH):
-                for e in range(2):
-                    nc.tensor.matmul(out=ps[:], lhsT=w_sb[:, c, e, :], rhs=xb[:, c, :, e], start=(c == 0 and e == 0), stop=False)
-            nc.tensor.matmul(out=ps[:], lhsT=wt_sb[:], rhs=xTt_t[b][:], start=False, stop=True)
-            zT_t[b] = work.tile([P, NODES], F32, name="zT_sb")
-            nc.scalar.activation(out=zT_t[b][:], in_=ps[:], func=ACT.Sigmoid, bias=bias_f[:, 0:1], scale=1.0)
+        def gate_mm(b, k):
+            if k == 0:
+                gps_t[b] = psum.tile([P, NODES], F32, name="G", tag="G")
+            if k < 2 * NCH:
+                xb = xT_t[b][:].bitcast(BF16).rearrange("p (c n e) -> p c n e", c=NCH, e=2)
+                nc.tensor.matmul(out=gps_t[b][:], lhsT=w_sb[:, k // 2, k % 2, :], rhs=xb[:, k // 2, :, k % 2], start=(k == 0), stop=False)
+            else:
+                nc.tensor.matmul(out=gps_t[b][:], lhsT=wt_sb[:], rhs=xTt_t[b][:], start=False, stop=True)
+                zT_t[b] = work.tile([P, NODES], F32, name="zT_sb")
+                nc.scalar.activation(out=zT_t[b][:], in_=gps_t[b][:], func=ACT.Sigmoid, bias=bias_f[:, 0:1], scale=1.0)
 
         def cgx(b):
             nc.vector.tensor_copy(out=cg[b % 2][:, 0:D, :], in_=xt_sb[:, b].rearrange("p t c -> p c t"))
 
         def zb_pe(b):
-            ps = bank("T", 4)
+            ps = bank()
             zps_t[b] = ps
             for t in range(T):
                 nc.tensor.transpose(ps[:, P * t:P * t + P], zT_t[b][:, P * t:P * t + P], ident_f[:])
@@ -147,38 +148,29 @@ def tile_dgggl_pa_t_kernel(tc, xg_gate, gate_w_z, gate_b_z, xt, state1, state2, 
         def dup(b):
             nc.vector.tensor_copy(out=stage_t[b][:, :, 3 * C:4 * C], in_=stage_t[b][:, :, 0:C])
 
-        def ta_pe(b, i):
+        def ta(b, i, h):
             aw = a_t[b][:, i, :].bitcast(F32).rearrange("p (j w) -> p j w", j=T)
-            for h in range(2):
-                ps = bank("T", 4)
-                aps_t[(b, i, h)] = ps
-                for u in range(2):
-                    for jj in range(2):
-                        j = 2 * h + jj
-                        if LAYOUT == "upe":
-                            src = aw[:, j, P * u:P * u + P]
-                        else:
-                            src = aw[:, j, :].rearrange("p (w u) -> p u w", u=2)[:, u, :]
-                        nc.tensor.transpose(ps[:, 256 * u + P * jj:256 * u + P * jj + P], src, ident_f[:])
-
-        def ta_exit(b, i, engines):
-            ag = work.tile([P, NODES * 2], F32, name="ag", bufs=3, align_bytes=64)
-            ag_t[(b, i)] = ag
-            for h in range(2):
-                src = aps_t[(b, i, h)][:].rearrange("p (u n) -> p n u", u=2)
-                dst = ag[:, 512 * h:512 * h + 512].rearrange("p (n u) -> p n u", u=2)
-                if engines[h] == "s":
-                    nc.scalar.copy(out=dst, in_=src)
-                else:
-                    nc.vector.tensor_copy(out=dst, in_=src)
+            ps = bank()
+            for u in range(2):
+                for jj in range(2):
+                    j = 2 * h + jj
+                    if LAYOUT == "upe":
+                        src = aw[:, j, P * u:P * u + P]
+                    else:
+                        src = aw[:, j, :].rearrange("p (w u) -> p u w", u=2)[:, u, :]
+                    nc.tensor.transpose(ps[:, 256 * u + P * jj:256 * u + P * jj + P], src, ident_f[:])
+            if h == 0:
+                ag_t[(b, i)] = work.tile([P, NODES * 2], F32, name="ag", bufs=3, align_bytes=64)
+            nc.scalar.copy(out=ag_t[(b, i)][:, 512 * h:512 * h + 512].rearrange("p (n u) -> p n u", u=2),
+                           in_=ps[:].rearrange("p (u n) -> p n u", u=2))
 
         def ta_quant(b, i):
-            ac_t[(b, i)] = work.tile([P, NODES], U32, name="a_codes", bufs=4, align_bytes=64)
-            as_t[(b, i)] = work.tile([P, NODES], U8, name="a_scales", bufs=4, align_bytes=64)
+            ac_t[(b, i)] = work.tile([P, NODES], U32, name="a_codes", bufs=6, align_bytes=64)
+            as_t[(b, i)] = work.tile([P, NODES], U8, name="a_scales", bufs=6, align_bytes=64)
             nc.vector.quantize_mx(out=ac_t[(b, i)][:].bitcast(FP8X4), scales=as_t[(b, i)][:], in_=ag_t[(b, i)][:].bitcast(BF16))
 
         def mx(b, i, h, codes, scales):
-            ps = bank("X", 3, F32, [P, 2, CP])
+            ps = bank(F32, [P, 2, CP])
             for jj in range(2):
                 j = 2 * h + jj
                 nc.tensor.matmul_mx(out=ps[:, jj, :], lhsT=ac_t[(b, i)][:, P * j:P * j + P].bitcast(FP8X4),
@@ -186,11 +178,10 @@ def tile_dgggl_pa_t_kernel(tc, xg_gate, gate_w_z, gate_b_z, xt, state1, state2, 
                                     rhs=codes[:].bitcast(FP8X4), rhs_scale=scales[:], start=True, stop=True)
             return ps
 
-        def x1(b, i):
+        def x1(b, i, h):
             o = 3 * C * i + C
-            for h in range(2):
-                ps = mx(b, i, h, cc_t[b], cs_t[b])
-                nc.scalar.copy(out=stage_t[b][:, 2 * h:2 * h + 2, o:o + C], in_=ps[:, :, 0:C])
+            ps = mx(b, i, h, cc_t[b], cs_t[b])
+            nc.scalar.copy(out=stage_t[b][:, 2 * h:2 * h + 2, o:o + C], in_=ps[:, :, 0:C])
 
         def x1_group(b, i):
             o = 3 * C * i + C
@@ -202,79 +193,67 @@ def tile_dgggl_pa_t_kernel(tc, xg_gate, gate_w_z, gate_b_z, xt, state1, state2, 
             ts_t[(b, i)] = work.tile([P, CP], U8, name="t_scales", bufs=4, align_bytes=64)
             nc.vector.quantize_mx(out=tc_t[(b, i)][:].bitcast(FP8X4), scales=ts_t[(b, i)][:], in_=g[:].rearrange("p c t -> p (c t)"))
 
-        def x2_pe(b, i, h):
-            xps_t[(b, i, h)] = mx(b, i, h, tc_t[(b, i)], ts_t[(b, i)])
-
-        def x2_exit(b, i, h):
+        def x2(b, i, h):
             o = 3 * C * i + 2 * C
-            nc.vector.scalar_tensor_tensor(out=stage_t[b][:, 2 * h:2 * h + 2, o:o + C], in0=xps_t[(b, i, h)][:, :, 0:C], scalar=2.0,
+            ps = mx(b, i, h, tc_t[(b, i)], ts_t[(b, i)])
+            nc.vector.scalar_tensor_tensor(out=stage_t[b][:, 2 * h:2 * h + 2, o:o + C], in0=ps[:, :, 0:C], scalar=2.0,
                                            in1=stage_t[b][:, 2 * h:2 * h + 2, 0:C], op0=ALU.mult, op1=ALU.subtract)
 
         def store(b, u):
             nc.sync.dma_start(out=nodes_view(out[b])[:, u, :], in_=stage_t[b][:, 2 * u:2 * u + 2, :].rearrange("p e f -> p (e f)"))
 
-        def late(b):
-            x2_exit(b, 0, 1)
-            x2_exit(b, 1, 1)
-            store(b, 1)
+        def ok(b):
+            return 0 <= b < B
 
         load_x(0)
         load_consts()
-        load_a(0)
         load_x(1)
-        load_states(0, 2)
-        load_a(1)
-        load_states(2, B)
-        load_x(2)
-        load_a(2)
-        cgx(0)
-        for pi in range(-2, B - 1):
-            b2, b1 = pi + 2, pi + 1
-            go2, go1 = b2 < B, b1 >= 0
-            if pi >= -1 and pi + 4 < B:
-                load_x(pi + 4)
+        for pi in range(-4, B):
+            b_t, b_g, b_a, b_z, b_1, b_0 = pi + 4, pi + 3, pi + 2, pi + 2, pi + 1, pi
+            if ok(pi + 6) and pi + 6 >= 2:
+                load_x(pi + 6)
+            if ok(pi + 4):
                 load_a(pi + 4)
-            if go2:
-                t1(b2, [0, 1])
-            if go1:
-                zb_pe(b1)
-                cand(b1)
-            if b1 >= 1:
-                late(b1 - 1)
-            if go2:
-                t1(b2, [2, 3, 4])
-                if pi == -2:
-                    gate(b2)
-                ta_pe(b2, 0)
-                ta_pe(b2, 1)
-            if go1:
-                if b1 + 1 < B:
-                    cgx(b1 + 1)
-            if go2:
-                ta_exit(b2, 0, "ss")
-            if go1:
-                x1(b1, 0)
-                x1(b1, 1)
-                x1_group(b1, 0)
-            if go2:
-                ta_quant(b2, 0)
-            if go1:
-                x1_quant(b1, 0)
-                x1_group(b1, 1)
-                dup(b1)
-                x1_quant(b1, 1)
-            if go2:
-                ta_exit(b2, 1, "ss")
-                if pi > -2:
-                    gate(b2)
-            if go1:
-                x2_pe(b1, 0, 0)
-                x2_pe(b1, 1, 0)
-                x2_exit(b1, 0, 0)
-                x2_exit(b1, 1, 0)
-                store(b1, 0)
-                x2_pe(b1, 0, 1)
-                x2_pe(b1, 1, 1)
-            if go2:
-                ta_quant(b2, 1)
-        late(B - 1)
+            if pi == -4:
+                load_states(0, 2)
+                cgx(0)
+            if pi == -3:
+                load_states(2, B)
+            if ok(b_0):
+                x1_group(b_0, 0)
+                x1_group(b_0, 1)
+                x1_quant(b_0, 0)
+                x1_quant(b_0, 1)
+            jobs = []
+            if ok(b_z):
+                jobs.append(("z", 0, 0))
+            if ok(b_a):
+                jobs.extend([("a", i, h) for i in range(NS) for h in range(2)])
+            if ok(b_t):
+                jobs.extend([("t", c, 0) for c in range(NCH + 1)])
+            n_mm = 2 * NCH + 1 if ok(b_g) else 0
+            for k in range(max(len(jobs), n_mm)):
+                if k < len(jobs):
+                    kind, q0, q1 = jobs[k]
+                    if kind == "z":
+                        zb_pe(b_z)
+                        cand(b_z)
+                        dup(b_z)
+                        if ok(b_z + 1):
+                            cgx(b_z + 1)
+                    elif kind == "a":
+                        ta(b_a, q0, q1)
+                        if q1 == 1:
+                            ta_quant(b_a, q0)
+                    else:
+                        t1(b_t, q0)
+                if k < n_mm:
+                    gate_mm(b_g, k)
+            for h in range(2):
+                for i in range(NS):
+                    if ok(b_0):
+                        x2(b_0, i, h)
+                    if ok(b_1):
+                        x1(b_1, i, h)
+                if ok(b_0):
+                    store(b_0, h)

@@ -21,7 +21,7 @@ FW = F // 2
 NCH = 4
 FLOPS = 2 * B * NODES * F * G + 2 * NS * 2 * B * NODES * NODES * C
 MANUAL = True
-LAYOUT = "upe"
+LAYOUT = "pt"
 NROT = 7
 
 
@@ -199,11 +199,19 @@ def tile_dgggl_pa_t_kernel(tc, xg_gate, gate_w_z, gate_b_z, xt, state1, state2, 
             nc.vector.scalar_tensor_tensor(out=stage_t[b][:, 2 * h:2 * h + 2, o:o + C], in0=ps[:, :, 0:C], scalar=2.0,
                                            in1=stage_t[b][:, 2 * h:2 * h + 2, 0:C], op0=ALU.mult, op1=ALU.subtract)
 
-        def store(b, u):
-            nc.sync.dma_start(out=nodes_view(out[b])[:, u, :], in_=stage_t[b][:, 2 * u:2 * u + 2, :].rearrange("p e f -> p (e f)"))
+        def store(b, u, lo, hi):
+            nc.sync.dma_start(out=nodes_view(out[b]).rearrange("p u (e f) -> p u e f", e=2)[:, u, :, lo:hi],
+                              in_=stage_t[b][:, 2 * u:2 * u + 2, lo:hi])
 
         def ok(b):
             return 0 <= b < B
+
+        left = {"mm": 0}
+
+        def one_gate_matmul(b):
+            if left["mm"] > 0:
+                gate_mm(b, 2 * NCH + 1 - left["mm"])
+                left["mm"] -= 1
 
         load_x(0)
         load_consts()
@@ -224,31 +232,29 @@ def tile_dgggl_pa_t_kernel(tc, xg_gate, gate_w_z, gate_b_z, xt, state1, state2, 
                 x1_group(b_0, 1)
                 x1_quant(b_0, 0)
                 x1_quant(b_0, 1)
-            jobs = []
+            left["mm"] = 2 * NCH + 1 if ok(b_g) else 0
+            if b_g == 0:
+                for k in range(2 * NCH + 1):
+                    one_gate_matmul(b_g)
             if ok(b_z):
-                jobs.append(("z", 0, 0))
+                zb_pe(b_z)
+                cand(b_z)
+                dup(b_z)
+                if ok(b_z + 1):
+                    cgx(b_z + 1)
+                one_gate_matmul(b_g)
             if ok(b_a):
-                jobs.extend([("a", i, h) for i in range(NS) for h in range(2)])
+                for i in range(NS):
+                    for h in range(2):
+                        ta(b_a, i, h)
+                        one_gate_matmul(b_g)
+                    ta_quant(b_a, i)
             if ok(b_t):
-                jobs.extend([("t", c, 0) for c in range(NCH + 1)])
-            n_mm = 2 * NCH + 1 if ok(b_g) else 0
-            for k in range(max(len(jobs), n_mm)):
-                if k < len(jobs):
-                    kind, q0, q1 = jobs[k]
-                    if kind == "z":
-                        zb_pe(b_z)
-                        cand(b_z)
-                        dup(b_z)
-                        if ok(b_z + 1):
-                            cgx(b_z + 1)
-                    elif kind == "a":
-                        ta(b_a, q0, q1)
-                        if q1 == 1:
-                            ta_quant(b_a, q0)
-                    else:
-                        t1(b_t, q0)
-                if k < n_mm:
-                    gate_mm(b_g, k)
+                for c in range(NCH + 1):
+                    t1(b_t, c)
+                    one_gate_matmul(b_g)
+            for k in range(2 * NCH + 1):
+                one_gate_matmul(b_g)
             for h in range(2):
                 for i in range(NS):
                     if ok(b_0):
@@ -256,4 +262,4 @@ def tile_dgggl_pa_t_kernel(tc, xg_gate, gate_w_z, gate_b_z, xt, state1, state2, 
                     if ok(b_1):
                         x1(b_1, i, h)
                 if ok(b_0):
-                    store(b_0, h)
+                    store(b_0, h, 0, F)

@@ -12,17 +12,22 @@ ALU = mybir.AluOpType
 ACT = mybir.ActivationFunctionType
 
 P = 128
-B, NODES, F, D, C = 8, 512, 1152, 64, 192
+B = 8
+NODES = 512
+SLOTS = NODES // P
+F = 1152
+D = 64
 G = 2 * D
+C = 3 * D
+C_PAD = 256
 NS = 2
-T = 4
-CP = 256
-FW = F // 2
-NCH = 4
+WORDS = F // 2
+CHUNKS = 4
+GATE_STEPS = 2 * CHUNKS + 1
+BANK = 512
+TURN_BANKS = 7
+
 FLOPS = 2 * B * NODES * F * G + 2 * NS * 2 * B * NODES * NODES * C
-MANUAL = True
-LAYOUT = "pt"
-NROT = 7
 
 
 def tile_dgggl_pa_t_kernel(tc, xg_gate, gate_w_z, gate_b_z, xt, state1, state2, supports, out):
@@ -31,235 +36,210 @@ def tile_dgggl_pa_t_kernel(tc, xg_gate, gate_w_z, gate_b_z, xt, state1, state2, 
         const = ctx.enter_context(tc.tile_pool(name="const", bufs=1))
         loads = ctx.enter_context(tc.tile_pool(name="loads", bufs=3))
         work = ctx.enter_context(tc.tile_pool(name="work", bufs=2))
-        stages = ctx.enter_context(tc.tile_pool(name="stages", bufs=4))
+        rows = ctx.enter_context(tc.tile_pool(name="rows", bufs=4))
         psum = ctx.enter_context(tc.psum_pool(name="psum", bufs=1))
-        if MANUAL:
-            ctx.enter_context(tc.manual_schedule())
-
-        def nodes_view(ap):
-            if LAYOUT == "upe":
-                return ap.rearrange("(u p e) f -> p u (e f)", u=2, e=2)
-            return ap.rearrange("(p u e) f -> p u (e f)", u=2, e=2)
+        ctx.enter_context(tc.manual_schedule())
 
         ident_f = const.tile([P, P], F32, name="ident_f")
         make_identity(nc, ident_f[:])
         ident_b = const.tile([P, P], BF16, name="ident_b")
         make_identity(nc, ident_b[:])
-        w_sb = const.tile([P, NCH, 2, G], BF16, name="w_sb")
-        wt_sb = const.tile([P, G], BF16, name="wt_sb")
+        w_sb = const.tile([P, CHUNKS, 2, G], BF16, name="w_sb")
+        w_tail = const.tile([P, G], BF16, name="w_tail")
         bias_b = const.tile([P, 1], BF16, name="bias_b")
         bias_f = const.tile([P, 1], F32, name="bias_f")
-        xt_sb = const.tile([P, B, T, D], BF16, name="xt_sb")
-        st_sb = const.tile([P, B, 2, T, D], BF16, name="st_sb")
-        cg = [const.tile([P, CP, T], BF16, name="cg%d" % k, align_bytes=64) for k in range(2)]
-        tg = [const.tile([P, CP, T], BF16, name="tg%d" % k, align_bytes=64) for k in range(4)]
-        for g in cg + tg:
-            nc.vector.memset(g[:, C:CP, :], 0.0)
+        xt_sb = const.tile([P, B, SLOTS, D], BF16, name="xt_sb")
+        st_sb = const.tile([P, B, 2, SLOTS, D], BF16, name="st_sb")
+        cand_grouped = [const.tile([P, C_PAD, SLOTS], BF16, name="cand_grouped%d" % k, align_bytes=64) for k in range(2)]
+        t1_grouped = [const.tile([P, C_PAD, SLOTS], BF16, name="t1_grouped%d" % k, align_bytes=64) for k in range(4)]
+        for grouped in cand_grouped + t1_grouped:
+            nc.vector.memset(grouped[:, C:C_PAD, :], 0.0)
 
-        xg_t, a_t, xT_t, xTt_t, zT_t, stage_t, zps_t, gps_t = {}, {}, {}, {}, {}, {}, {}, {}
-        cc_t, cs_t, ac_t, as_t, tc_t, ts_t, aps_t, ag_t, xps_t = {}, {}, {}, {}, {}, {}, {}, {}, {}
-        cnt = {"R": 0}
+        xg_sb, a_sb, x_t, x_t_tail, gate_ps, z_t, z_ps, row = {}, {}, {}, {}, {}, {}, {}, {}
+        a_grouped, a_codes, a_scales, cand_codes, cand_scales, t1_codes, t1_scales = {}, {}, {}, {}, {}, {}, {}
+        turn = {"bank": 0, "gate_steps_left": 0}
 
-        def bank(dtype=F32, shape=None):
-            k = cnt["R"] % NROT
-            cnt["R"] += 1
-            return psum.tile(shape or [P, 512], dtype, name="R%d" % k, tag="R%d" % k)
+        def next_bank(shape, dtype):
+            k = turn["bank"] % TURN_BANKS
+            turn["bank"] += 1
+            return psum.tile(shape, dtype, name="turn%d" % k, tag="turn%d" % k)
 
-        def load_x(b):
-            xg_sb = loads.tile([P, T * F], BF16, name="xg_sb")
-            xg_t[b] = xg_sb
-            nc.sync.dma_start(out=xg_sb[:].rearrange("p (u x) -> p u x", u=2), in_=nodes_view(xg_gate[b]))
+        def work_order(ap):
+            return ap.rearrange("(u p e) f -> p u e f", u=2, e=2)
 
-        def load_a(b):
-            a_sb = loads.tile([P, NS, T * NODES], BF16, name="a_sb")
-            a_t[b] = a_sb
+        def load_xg(b):
+            xg_sb[b] = loads.tile([P, SLOTS * F], BF16, name="xg_sb")
+            nc.sync.dma_start(out=xg_sb[b][:], in_=xg_gate[b].rearrange("(p j) f -> p (j f)", j=SLOTS))
+
+        def load_supports(b):
+            a_sb[b] = loads.tile([P, NS, SLOTS * NODES], BF16, name="a_sb")
             for i in range(NS):
-                nc.sync.dma_start(out=a_sb[:, i, :].rearrange("p (u x) -> p u x", u=2), in_=nodes_view(supports[i, b]))
+                nc.sync.dma_start(out=a_sb[b][:, i, :], in_=supports[i, b].rearrange("(p j) m -> p (j m)", j=SLOTS))
 
-        def load_consts():
-            nc.sync.dma_start(out=w_sb[:].rearrange("p c e g -> p c (e g)"),
-                              in_=gate_w_z[0:NCH * 2 * P, :].rearrange("(c w e) g -> w c (e g)", c=NCH, e=2))
-            nc.sync.dma_start(out=wt_sb[:], in_=gate_w_z[NCH * 2 * P:F, :])
+        def load_weights():
+            nc.sync.dma_start(out=w_sb[:].rearrange("w c e g -> w c (e g)"),
+                              in_=gate_w_z[0:2 * P * CHUNKS, :].rearrange("(c w e) g -> w c (e g)", c=CHUNKS, e=2))
+            nc.sync.dma_start(out=w_tail[:], in_=gate_w_z[2 * P * CHUNKS:F, :])
             with nc.allow_non_contiguous_dma(reason="one bias value to a partition"):
                 nc.sync.dma_start(out=bias_b[:], in_=gate_b_z.rearrange("(g o) -> g o", o=1))
             nc.vector.tensor_copy(out=bias_f[:], in_=bias_b[:])
 
-        def load_states(b0, b1):
-            srcs = ((xt, xt_sb[:, b0:b1]), (state1, st_sb[:, b0:b1, 0]), (state2, st_sb[:, b0:b1, 1]))
-            if LAYOUT == "upe":
-                for u in range(2):
-                    for src, dst in srcs:
-                        nc.sync.dma_start(out=dst[:, :, 2 * u:2 * u + 2, :].rearrange("p b e d -> p b (e d)"),
-                                          in_=src[b0:b1].rearrange("b (u p e) d -> u p b (e d)", u=2, e=2)[u])
-            else:
-                for src, dst in srcs:
-                    nc.sync.dma_start(out=dst.rearrange("p b t d -> p b (t d)"),
-                                      in_=src[b0:b1].rearrange("b (p t) d -> p b (t d)", t=T))
-
-        def t1(b, c):
-            if b not in xT_t:
-                xT_t[b] = work.tile([P, NCH * NODES], F32, name="xT_sb")
-                xTt_t[b] = work.tile([P, NODES], BF16, name="xTt_sb")
-            xw = xg_t[b][:].bitcast(F32)
-            if c < NCH:
-                ps = bank()
-                for t in range(T):
-                    nc.tensor.transpose(ps[:, P * t:P * t + P], xw[:, FW * t + P * c:FW * t + P * c + P], ident_f[:])
-                nc.scalar.copy(out=xT_t[b][:, NODES * c:NODES * c + NODES], in_=ps[:])
-            else:
-                ps = bank(BF16)
-                for t in range(T):
-                    nc.tensor.transpose(ps[:, P * t:P * t + P], xg_t[b][:, F * t + 2 * P * NCH:F * t + F], ident_b[:])
-                nc.scalar.copy(out=xTt_t[b][:], in_=ps[:])
-
-        def gate_mm(b, k):
-            if k == 0:
-                gps_t[b] = psum.tile([P, NODES], F32, name="G", tag="G")
-            if k < 2 * NCH:
-                xb = xT_t[b][:].bitcast(BF16).rearrange("p (c n e) -> p c n e", c=NCH, e=2)
-                nc.tensor.matmul(out=gps_t[b][:], lhsT=w_sb[:, k // 2, k % 2, :], rhs=xb[:, k // 2, :, k % 2], start=(k == 0), stop=False)
-            else:
-                nc.tensor.matmul(out=gps_t[b][:], lhsT=wt_sb[:], rhs=xTt_t[b][:], start=False, stop=True)
-                zT_t[b] = work.tile([P, NODES], F32, name="zT_sb")
-                nc.scalar.activation(out=zT_t[b][:], in_=gps_t[b][:], func=ACT.Sigmoid, bias=bias_f[:, 0:1], scale=1.0)
-
-        def cgx(b):
-            nc.vector.tensor_copy(out=cg[b % 2][:, 0:D, :], in_=xt_sb[:, b].rearrange("p t c -> p c t"))
-
-        def zb_pe(b):
-            ps = bank()
-            zps_t[b] = ps
-            for t in range(T):
-                nc.tensor.transpose(ps[:, P * t:P * t + P], zT_t[b][:, P * t:P * t + P], ident_f[:])
-
-        def cand(b):
-            stage = stages.tile([P, T, F], F32, name="stage")
-            stage_t[b] = stage
-            nc.vector.tensor_tensor(out=stage[:, :, D:C].rearrange("p t (s d) -> p t s d", s=2),
-                                    in0=zps_t[b][:].rearrange("p (t s d) -> p t s d", t=T, s=2),
-                                    in1=st_sb[:, b].rearrange("p s t d -> p t s d"), op=ALU.mult)
-            g = cg[b % 2]
-            nc.vector.tensor_copy(out=g[:, D:C, :], in_=stage[:, :, D:C].rearrange("p t c -> p c t"))
-            nc.vector.tensor_copy(out=stage[:, :, 0:D], in_=xt_sb[:, b])
-            cc_t[b] = work.tile([P, CP], U32, name="c_codes", align_bytes=64)
-            cs_t[b] = work.tile([P, CP], U8, name="c_scales", align_bytes=64)
-            nc.vector.quantize_mx(out=cc_t[b][:].bitcast(FP8X4), scales=cs_t[b][:], in_=g[:].rearrange("p c t -> p (c t)"))
-
-        def dup(b):
-            nc.vector.tensor_copy(out=stage_t[b][:, :, 3 * C:4 * C], in_=stage_t[b][:, :, 0:C])
-
-        def ta(b, i, h):
-            aw = a_t[b][:, i, :].bitcast(F32).rearrange("p (j w) -> p j w", j=T)
-            ps = bank()
+        def load_states(b_from, b_to):
+            pairs = ((xt, xt_sb[:, b_from:b_to]), (state1, st_sb[:, b_from:b_to, 0]), (state2, st_sb[:, b_from:b_to, 1]))
             for u in range(2):
-                for jj in range(2):
-                    j = 2 * h + jj
-                    if LAYOUT == "upe":
-                        src = aw[:, j, P * u:P * u + P]
-                    else:
-                        src = aw[:, j, :].rearrange("p (w u) -> p u w", u=2)[:, u, :]
-                    nc.tensor.transpose(ps[:, 256 * u + P * jj:256 * u + P * jj + P], src, ident_f[:])
-            if h == 0:
-                ag_t[(b, i)] = work.tile([P, NODES * 2], F32, name="ag", bufs=3, align_bytes=64)
-            nc.scalar.copy(out=ag_t[(b, i)][:, 512 * h:512 * h + 512].rearrange("p (n u) -> p n u", u=2),
-                           in_=ps[:].rearrange("p (u n) -> p n u", u=2))
+                for src, dst in pairs:
+                    nc.sync.dma_start(out=dst[:, :, 2 * u:2 * u + 2, :].rearrange("p b e d -> p b (e d)"),
+                                      in_=src[b_from:b_to].rearrange("b (u p e) d -> u p b (e d)", u=2, e=2)[u])
 
-        def ta_quant(b, i):
-            ac_t[(b, i)] = work.tile([P, NODES], U32, name="a_codes", bufs=6, align_bytes=64)
-            as_t[(b, i)] = work.tile([P, NODES], U8, name="a_scales", bufs=6, align_bytes=64)
-            nc.vector.quantize_mx(out=ac_t[(b, i)][:].bitcast(FP8X4), scales=as_t[(b, i)][:], in_=ag_t[(b, i)][:].bitcast(BF16))
+        def transpose_xg(b, c):
+            if c == 0:
+                x_t[b] = work.tile([P, CHUNKS * NODES], F32, name="x_t")
+                x_t_tail[b] = work.tile([P, NODES], BF16, name="x_t_tail")
+            if c < CHUNKS:
+                words = xg_sb[b][:].bitcast(F32)
+                ps = next_bank([P, BANK], F32)
+                for j in range(SLOTS):
+                    nc.tensor.transpose(ps[:, P * j:P * j + P], words[:, WORDS * j + P * c:WORDS * j + P * c + P], ident_f[:])
+                nc.scalar.copy(out=x_t[b][:, NODES * c:NODES * c + NODES], in_=ps[:])
+            else:
+                ps = next_bank([P, NODES], BF16)
+                for j in range(SLOTS):
+                    nc.tensor.transpose(ps[:, P * j:P * j + P], xg_sb[b][:, F * j + 2 * P * CHUNKS:F * j + F], ident_b[:])
+                nc.scalar.copy(out=x_t_tail[b][:], in_=ps[:])
 
-        def mx(b, i, h, codes, scales):
-            ps = bank(F32, [P, 2, CP])
-            for jj in range(2):
-                j = 2 * h + jj
-                nc.tensor.matmul_mx(out=ps[:, jj, :], lhsT=ac_t[(b, i)][:, P * j:P * j + P].bitcast(FP8X4),
-                                    lhsT_scale=as_t[(b, i)][:, P * j:P * j + P],
+        def gate_step(b):
+            if turn["gate_steps_left"] == 0:
+                return
+            k = GATE_STEPS - turn["gate_steps_left"]
+            turn["gate_steps_left"] -= 1
+            if k == 0:
+                gate_ps[b] = psum.tile([P, NODES], F32, name="gate_ps", tag="gate_ps")
+            if k < 2 * CHUNKS:
+                halves = x_t[b][:].bitcast(BF16).rearrange("w (c n e) -> w c n e", c=CHUNKS, e=2)
+                nc.tensor.matmul(out=gate_ps[b][:], lhsT=w_sb[:, k // 2, k % 2, :], rhs=halves[:, k // 2, :, k % 2],
+                                 start=(k == 0), stop=False)
+                return
+            nc.tensor.matmul(out=gate_ps[b][:], lhsT=w_tail[:], rhs=x_t_tail[b][:], start=False, stop=True)
+            z_t[b] = work.tile([P, NODES], F32, name="z_t")
+            nc.scalar.activation(out=z_t[b][:].rearrange("g (e n q) -> g e n q", e=2, q=2),
+                                 in_=gate_ps[b][:].rearrange("g (q e n) -> g e n q", q=2, e=2),
+                                 func=ACT.Sigmoid, bias=bias_f[:, 0:1], scale=1.0)
+
+        def group_xt(b):
+            nc.vector.tensor_copy(out=cand_grouped[b % 2][:, 0:D, :], in_=xt_sb[:, b].rearrange("p t c -> p c t"))
+
+        def candidate(b):
+            z_ps[b] = next_bank([P, BANK], F32)
+            for t in range(SLOTS):
+                first = 256 * (t % 2) + P * (t // 2)
+                nc.tensor.transpose(z_ps[b][:, P * t:P * t + P], z_t[b][:, first:first + P], ident_f[:])
+            row[b] = rows.tile([P, SLOTS, F], F32, name="row")
+            nc.vector.tensor_tensor(out=row[b][:, :, D:C].rearrange("p t (s d) -> p t s d", s=2),
+                                    in0=z_ps[b][:].rearrange("p (t s d) -> p t s d", t=SLOTS, s=2),
+                                    in1=st_sb[:, b].rearrange("p s t d -> p t s d"), op=ALU.mult)
+            grouped = cand_grouped[b % 2]
+            nc.vector.tensor_copy(out=grouped[:, D:C, :], in_=row[b][:, :, D:C].rearrange("p t c -> p c t"))
+            nc.vector.tensor_copy(out=row[b][:, :, 0:D], in_=xt_sb[:, b])
+            cand_codes[b] = work.tile([P, C_PAD], U32, name="cand_codes", align_bytes=64)
+            cand_scales[b] = work.tile([P, C_PAD], U8, name="cand_scales", align_bytes=64)
+            nc.vector.quantize_mx(out=cand_codes[b][:].bitcast(FP8X4), scales=cand_scales[b][:],
+                                  in_=grouped[:].rearrange("p c t -> p (c t)"))
+            nc.vector.tensor_copy(out=row[b][:, :, 3 * C:4 * C], in_=row[b][:, :, 0:C])
+            if b + 1 < B:
+                group_xt(b + 1)
+
+        def transpose_supports(b, i, e):
+            words = a_sb[b][:, i, :].bitcast(F32).rearrange("p (j w) -> p j w", j=SLOTS)
+            ps = next_bank([P, BANK], F32)
+            for v in range(2):
+                for q in range(2):
+                    nc.tensor.transpose(ps[:, 256 * v + P * q:256 * v + P * q + P], words[:, 2 * q + e, P * v:P * v + P], ident_f[:])
+            if e == 0:
+                a_grouped[(b, i)] = work.tile([P, 2 * NODES], F32, name="a_grouped", bufs=3, align_bytes=64)
+            nc.scalar.copy(out=a_grouped[(b, i)][:, BANK * e:BANK * e + BANK].rearrange("w (n q v) -> w n q v", q=2, v=2),
+                           in_=ps[:].rearrange("w (v q n) -> w n q v", v=2, q=2))
+
+        def quantise_supports(b, i):
+            a_codes[(b, i)] = work.tile([P, NODES], U32, name="a_codes", bufs=6, align_bytes=64)
+            a_scales[(b, i)] = work.tile([P, NODES], U8, name="a_scales", bufs=6, align_bytes=64)
+            nc.vector.quantize_mx(out=a_codes[(b, i)][:].bitcast(FP8X4), scales=a_scales[(b, i)][:],
+                                  in_=a_grouped[(b, i)][:].bitcast(BF16))
+
+        def mx_product(b, i, u, codes, scales):
+            ps = next_bank([P, 2, C_PAD], F32)
+            for e in range(2):
+                first = 256 * e + P * u
+                nc.tensor.matmul_mx(out=ps[:, e, :], lhsT=a_codes[(b, i)][:, first:first + P].bitcast(FP8X4),
+                                    lhsT_scale=a_scales[(b, i)][:, first:first + P],
                                     rhs=codes[:].bitcast(FP8X4), rhs_scale=scales[:], start=True, stop=True)
             return ps
 
-        def x1(b, i, h):
-            o = 3 * C * i + C
-            ps = mx(b, i, h, cc_t[b], cs_t[b])
-            nc.scalar.copy(out=stage_t[b][:, 2 * h:2 * h + 2, o:o + C], in_=ps[:, :, 0:C])
+        def first_product(b, i, u):
+            ps = mx_product(b, i, u, cand_codes[b], cand_scales[b])
+            first = 3 * C * i + C
+            nc.scalar.copy(out=row[b][:, 2 * u:2 * u + 2, first:first + C], in_=ps[:, :, 0:C])
 
-        def x1_group(b, i):
-            o = 3 * C * i + C
-            nc.vector.tensor_copy(out=tg[(2 * b + i) % 4][:, 0:C, :], in_=stage_t[b][:, :, o:o + C].rearrange("p t c -> p c t"))
+        def quantise_t1(b):
+            for i in range(NS):
+                first = 3 * C * i + C
+                nc.vector.tensor_copy(out=t1_grouped[(2 * b + i) % 4][:, 0:C, :],
+                                      in_=row[b][:, :, first:first + C].rearrange("p t c -> p c t"))
+            for i in range(NS):
+                t1_codes[(b, i)] = work.tile([P, C_PAD], U32, name="t1_codes", bufs=4, align_bytes=64)
+                t1_scales[(b, i)] = work.tile([P, C_PAD], U8, name="t1_scales", bufs=4, align_bytes=64)
+                nc.vector.quantize_mx(out=t1_codes[(b, i)][:].bitcast(FP8X4), scales=t1_scales[(b, i)][:],
+                                      in_=t1_grouped[(2 * b + i) % 4][:].rearrange("p c t -> p (c t)"))
 
-        def x1_quant(b, i):
-            g = tg[(2 * b + i) % 4]
-            tc_t[(b, i)] = work.tile([P, CP], U32, name="t_codes", bufs=4, align_bytes=64)
-            ts_t[(b, i)] = work.tile([P, CP], U8, name="t_scales", bufs=4, align_bytes=64)
-            nc.vector.quantize_mx(out=tc_t[(b, i)][:].bitcast(FP8X4), scales=ts_t[(b, i)][:], in_=g[:].rearrange("p c t -> p (c t)"))
+        def second_product(b, i, u):
+            ps = mx_product(b, i, u, t1_codes[(b, i)], t1_scales[(b, i)])
+            first = 3 * C * i + 2 * C
+            nc.vector.scalar_tensor_tensor(out=row[b][:, 2 * u:2 * u + 2, first:first + C], in0=ps[:, :, 0:C], scalar=2.0,
+                                           in1=row[b][:, 2 * u:2 * u + 2, 0:C], op0=ALU.mult, op1=ALU.subtract)
 
-        def x2(b, i, h):
-            o = 3 * C * i + 2 * C
-            ps = mx(b, i, h, tc_t[(b, i)], ts_t[(b, i)])
-            nc.vector.scalar_tensor_tensor(out=stage_t[b][:, 2 * h:2 * h + 2, o:o + C], in0=ps[:, :, 0:C], scalar=2.0,
-                                           in1=stage_t[b][:, 2 * h:2 * h + 2, 0:C], op0=ALU.mult, op1=ALU.subtract)
+        def store(b, u):
+            nc.sync.dma_start(out=work_order(out[b])[:, u], in_=row[b][:, 2 * u:2 * u + 2, :])
 
-        def store(b, u, lo, hi):
-            nc.sync.dma_start(out=nodes_view(out[b]).rearrange("p u (e f) -> p u e f", e=2)[:, u, :, lo:hi],
-                              in_=stage_t[b][:, 2 * u:2 * u + 2, lo:hi])
-
-        def ok(b):
+        def exists(b):
             return 0 <= b < B
 
-        left = {"mm": 0}
-
-        def one_gate_matmul(b):
-            if left["mm"] > 0:
-                gate_mm(b, 2 * NCH + 1 - left["mm"])
-                left["mm"] -= 1
-
-        load_x(0)
-        load_consts()
-        load_x(1)
-        for pi in range(-4, B):
-            b_t, b_g, b_a, b_z, b_1, b_0 = pi + 4, pi + 3, pi + 2, pi + 2, pi + 1, pi
-            if ok(pi + 6) and pi + 6 >= 2:
-                load_x(pi + 6)
-            if ok(pi + 4):
-                load_a(pi + 4)
-            if pi == -4:
+        load_xg(0)
+        load_weights()
+        load_xg(1)
+        for n in range(-4, B):
+            if exists(n + 6) and n + 6 >= 2:
+                load_xg(n + 6)
+            if exists(n + 4):
+                load_supports(n + 4)
+            if n == -4:
                 load_states(0, 2)
-                cgx(0)
-            if pi == -3:
+                group_xt(0)
+            if n == -3:
                 load_states(2, B)
-            if ok(b_0):
-                x1_group(b_0, 0)
-                x1_group(b_0, 1)
-                x1_quant(b_0, 0)
-                x1_quant(b_0, 1)
-            left["mm"] = 2 * NCH + 1 if ok(b_g) else 0
-            if b_g == 0:
-                for k in range(2 * NCH + 1):
-                    one_gate_matmul(b_g)
-            if ok(b_z):
-                zb_pe(b_z)
-                cand(b_z)
-                dup(b_z)
-                if ok(b_z + 1):
-                    cgx(b_z + 1)
-                one_gate_matmul(b_g)
-            if ok(b_a):
+            if exists(n):
+                quantise_t1(n)
+            turn["gate_steps_left"] = GATE_STEPS if exists(n + 3) else 0
+            if n + 3 == 0:
+                for k in range(GATE_STEPS):
+                    gate_step(n + 3)
+            if exists(n + 2):
+                candidate(n + 2)
+                gate_step(n + 3)
                 for i in range(NS):
-                    for h in range(2):
-                        ta(b_a, i, h)
-                        one_gate_matmul(b_g)
-                    ta_quant(b_a, i)
-            if ok(b_t):
-                for c in range(NCH + 1):
-                    t1(b_t, c)
-                    one_gate_matmul(b_g)
-            for k in range(2 * NCH + 1):
-                one_gate_matmul(b_g)
-            for h in range(2):
+                    for e in range(2):
+                        transpose_supports(n + 2, i, e)
+                        gate_step(n + 3)
+                    quantise_supports(n + 2, i)
+            if exists(n + 4):
+                for c in range(CHUNKS + 1):
+                    transpose_xg(n + 4, c)
+                    gate_step(n + 3)
+            for k in range(GATE_STEPS):
+                gate_step(n + 3)
+            for u in range(2):
                 for i in range(NS):
-                    if ok(b_0):
-                        x2(b_0, i, h)
-                    if ok(b_1):
-                        x1(b_1, i, h)
-                if ok(b_0):
-                    store(b_0, h, 0, F)
+                    if exists(n):
+                        second_product(n, i, u)
+                    if exists(n + 1):
+                        first_product(n + 1, i, u)
+                if exists(n):
+                    store(n, u)

@@ -206,10 +206,10 @@ def tile_dgggl_pa_t_kernel(tc, xg_gate, gate_w_z, gate_b_z, xt, state1, state2, 
         load_weights()
         load_xg(1)
         for n in range(-4, B):
-            if exists(n + 6) and n + 6 >= 2:
-                load_xg(n + 6)
             if exists(n + 4):
                 load_supports(n + 4)
+            if exists(n + 6) and n + 6 >= 2:
+                load_xg(n + 6)
             if n == -4:
                 load_states(0, 2)
                 group_xt(0)

@@ -15,6 +15,7 @@ P = 128
 B = 8
 NODES = 512
 SLOTS = NODES // P
+HALF = NODES // 2
 F = 1152
 D = 64
 G = 2 * D
@@ -25,6 +26,7 @@ WORDS = F // 2
 CHUNKS = 4
 GATE_STEPS = 2 * CHUNKS + 1
 BANK = 512
+RUN = 4
 TURN_BANKS = 7
 
 FLOPS = 2 * B * NODES * F * G + 2 * NS * 2 * B * NODES * NODES * C
@@ -51,21 +53,22 @@ def tile_dgggl_pa_t_kernel(tc, xg_gate, gate_w_z, gate_b_z, xt, state1, state2, 
         xt_sb = const.tile([P, B, SLOTS, D], BF16, name="xt_sb")
         st_sb = const.tile([P, B, 2, SLOTS, D], BF16, name="st_sb")
         cand_grouped = [const.tile([P, C_PAD, SLOTS], BF16, name="cand_grouped%d" % k, align_bytes=64) for k in range(2)]
-        t1_grouped = [const.tile([P, C_PAD, SLOTS], BF16, name="t1_grouped%d" % k, align_bytes=64) for k in range(4)]
+        t1_grouped = [const.tile([P, C_PAD, SLOTS], BF16, name="t1_grouped%d" % k, align_bytes=64) for k in range(2 * NS)]
         for grouped in cand_grouped + t1_grouped:
             nc.vector.memset(grouped[:, C:C_PAD, :], 0.0)
 
         xg_sb, a_sb, x_t, x_t_tail, gate_ps, z_t, z_ps, row = {}, {}, {}, {}, {}, {}, {}, {}
         a_grouped, a_codes, a_scales, cand_codes, cand_scales, t1_codes, t1_scales = {}, {}, {}, {}, {}, {}, {}
-        turn = {"bank": 0, "gate_steps_left": 0}
+        count = {"banks_taken": 0, "gate_steps_left": 0}
 
         def next_bank(shape, dtype):
-            k = turn["bank"] % TURN_BANKS
-            turn["bank"] += 1
+            k = count["banks_taken"] % TURN_BANKS
+            count["banks_taken"] += 1
             return psum.tile(shape, dtype, name="turn%d" % k, tag="turn%d" % k)
 
-        def work_order(ap):
-            return ap.rearrange("(u p e) f -> p u e f", u=2, e=2)
+        def regroup(grouped_columns, slot_columns):
+            nc.vector.tensor_copy(out=grouped_columns.rearrange("p (c r) t -> p c t r", r=RUN),
+                                  in_=slot_columns.rearrange("p t (c r) -> p c t r", r=RUN))
 
         def load_xg(b):
             xg_sb[b] = loads.tile([P, SLOTS * F], BF16, name="xg_sb")
@@ -77,8 +80,8 @@ def tile_dgggl_pa_t_kernel(tc, xg_gate, gate_w_z, gate_b_z, xt, state1, state2, 
                 nc.sync.dma_start(out=a_sb[b][:, i, :], in_=supports[i, b].rearrange("(p j) m -> p (j m)", j=SLOTS))
 
         def load_weights():
-            nc.sync.dma_start(out=w_sb[:].rearrange("w c e g -> w c (e g)"),
-                              in_=gate_w_z[0:2 * P * CHUNKS, :].rearrange("(c w e) g -> w c (e g)", c=CHUNKS, e=2))
+            nc.sync.dma_start(out=w_sb[:].rearrange("w h r g -> w h (r g)"),
+                              in_=gate_w_z[0:2 * P * CHUNKS, :].rearrange("(h w r) g -> w h (r g)", h=CHUNKS, r=2))
             nc.sync.dma_start(out=w_tail[:], in_=gate_w_z[2 * P * CHUNKS:F, :])
             with nc.allow_non_contiguous_dma(reason="one bias value to a partition"):
                 nc.sync.dma_start(out=bias_b[:], in_=gate_b_z.rearrange("(g o) -> g o", o=1))
@@ -91,16 +94,17 @@ def tile_dgggl_pa_t_kernel(tc, xg_gate, gate_w_z, gate_b_z, xt, state1, state2, 
                     nc.sync.dma_start(out=dst[:, :, 2 * u:2 * u + 2, :].rearrange("p b e d -> p b (e d)"),
                                       in_=src[b_from:b_to].rearrange("b (u p e) d -> u p b (e d)", u=2, e=2)[u])
 
-        def transpose_xg(b, c):
-            if c == 0:
+        def transpose_xg(b, chunk):
+            if chunk == 0:
                 x_t[b] = work.tile([P, CHUNKS * NODES], F32, name="x_t")
                 x_t_tail[b] = work.tile([P, NODES], BF16, name="x_t_tail")
-            if c < CHUNKS:
+            if chunk < CHUNKS:
                 words = xg_sb[b][:].bitcast(F32)
                 ps = next_bank([P, BANK], F32)
                 for j in range(SLOTS):
-                    nc.tensor.transpose(ps[:, P * j:P * j + P], words[:, WORDS * j + P * c:WORDS * j + P * c + P], ident_f[:])
-                nc.scalar.copy(out=x_t[b][:, NODES * c:NODES * c + NODES], in_=ps[:])
+                    first = WORDS * j + P * chunk
+                    nc.tensor.transpose(ps[:, P * j:P * j + P], words[:, first:first + P], ident_f[:])
+                nc.scalar.copy(out=x_t[b][:, NODES * chunk:NODES * chunk + NODES], in_=ps[:])
             else:
                 ps = next_bank([P, NODES], BF16)
                 for j in range(SLOTS):
@@ -108,37 +112,38 @@ def tile_dgggl_pa_t_kernel(tc, xg_gate, gate_w_z, gate_b_z, xt, state1, state2, 
                 nc.scalar.copy(out=x_t_tail[b][:], in_=ps[:])
 
         def gate_step(b):
-            if turn["gate_steps_left"] == 0:
+            if count["gate_steps_left"] == 0:
                 return
-            k = GATE_STEPS - turn["gate_steps_left"]
-            turn["gate_steps_left"] -= 1
-            if k == 0:
+            step = GATE_STEPS - count["gate_steps_left"]
+            count["gate_steps_left"] -= 1
+            if step == 0:
                 gate_ps[b] = psum.tile([P, NODES], F32, name="gate_ps", tag="gate_ps")
-            if k < 2 * CHUNKS:
-                halves = x_t[b][:].bitcast(BF16).rearrange("w (c n e) -> w c n e", c=CHUNKS, e=2)
-                nc.tensor.matmul(out=gate_ps[b][:], lhsT=w_sb[:, k // 2, k % 2, :], rhs=halves[:, k // 2, :, k % 2],
-                                 start=(k == 0), stop=False)
+            if step < 2 * CHUNKS:
+                chunk, r = step // 2, step % 2
+                halves = x_t[b][:].bitcast(BF16).rearrange("w (h x r) -> w h x r", h=CHUNKS, r=2)
+                nc.tensor.matmul(out=gate_ps[b][:], lhsT=w_sb[:, chunk, r, :], rhs=halves[:, chunk, :, r],
+                                 start=(step == 0), stop=False)
                 return
             nc.tensor.matmul(out=gate_ps[b][:], lhsT=w_tail[:], rhs=x_t_tail[b][:], start=False, stop=True)
             z_t[b] = work.tile([P, NODES], F32, name="z_t")
-            nc.scalar.activation(out=z_t[b][:].rearrange("g (e n q) -> g e n q", e=2, q=2),
-                                 in_=gate_ps[b][:].rearrange("g (q e n) -> g e n q", q=2, e=2),
+            nc.scalar.activation(out=z_t[b][:].rearrange("g (e p q) -> g e p q", e=2, q=2),
+                                 in_=gate_ps[b][:].rearrange("g (q e p) -> g e p q", q=2, e=2),
                                  func=ACT.Sigmoid, bias=bias_f[:, 0:1], scale=1.0)
 
         def group_xt(b):
-            nc.vector.tensor_copy(out=cand_grouped[b % 2][:, 0:D, :], in_=xt_sb[:, b].rearrange("p t c -> p c t"))
+            regroup(cand_grouped[b % 2][:, 0:D, :], xt_sb[:, b])
 
         def candidate(b):
             z_ps[b] = next_bank([P, BANK], F32)
             for t in range(SLOTS):
-                first = 256 * (t % 2) + P * (t // 2)
+                first = HALF * (t % 2) + P * (t // 2)
                 nc.tensor.transpose(z_ps[b][:, P * t:P * t + P], z_t[b][:, first:first + P], ident_f[:])
             row[b] = rows.tile([P, SLOTS, F], F32, name="row")
             nc.vector.tensor_tensor(out=row[b][:, :, D:C].rearrange("p t (s d) -> p t s d", s=2),
                                     in0=z_ps[b][:].rearrange("p (t s d) -> p t s d", t=SLOTS, s=2),
                                     in1=st_sb[:, b].rearrange("p s t d -> p t s d"), op=ALU.mult)
             grouped = cand_grouped[b % 2]
-            nc.vector.tensor_copy(out=grouped[:, D:C, :], in_=row[b][:, :, D:C].rearrange("p t c -> p c t"))
+            regroup(grouped[:, D:C, :], row[b][:, :, D:C])
             nc.vector.tensor_copy(out=row[b][:, :, 0:D], in_=xt_sb[:, b])
             cand_codes[b] = work.tile([P, C_PAD], U32, name="cand_codes", align_bytes=64)
             cand_scales[b] = work.tile([P, C_PAD], U8, name="cand_scales", align_bytes=64)
@@ -153,24 +158,26 @@ def tile_dgggl_pa_t_kernel(tc, xg_gate, gate_w_z, gate_b_z, xt, state1, state2, 
             ps = next_bank([P, BANK], F32)
             for v in range(2):
                 for q in range(2):
-                    nc.tensor.transpose(ps[:, 256 * v + P * q:256 * v + P * q + P], words[:, 2 * q + e, P * v:P * v + P], ident_f[:])
-            if e == 0:
-                a_grouped[(b, i)] = work.tile([P, 2 * NODES], F32, name="a_grouped", bufs=3, align_bytes=64)
-            nc.scalar.copy(out=a_grouped[(b, i)][:, BANK * e:BANK * e + BANK].rearrange("w (n q v) -> w n q v", q=2, v=2),
-                           in_=ps[:].rearrange("w (v q n) -> w n q v", v=2, q=2))
+                    first = HALF * v + P * q
+                    nc.tensor.transpose(ps[:, first:first + P], words[:, 2 * q + e, P * v:P * v + P], ident_f[:])
+            if i == 0 and e == 0:
+                a_grouped[b] = work.tile([P, NS, 2 * NODES], F32, name="a_grouped", align_bytes=64)
+            nc.scalar.copy(out=a_grouped[b][:, i, BANK * e:BANK * e + BANK].rearrange("w (p q v) -> w p q v", q=2, v=2),
+                           in_=ps[:].rearrange("w (v q p) -> w p q v", v=2, q=2))
 
-        def quantise_supports(b, i):
-            a_codes[(b, i)] = work.tile([P, NODES], U32, name="a_codes", bufs=6, align_bytes=64)
-            a_scales[(b, i)] = work.tile([P, NODES], U8, name="a_scales", bufs=6, align_bytes=64)
-            nc.vector.quantize_mx(out=a_codes[(b, i)][:].bitcast(FP8X4), scales=a_scales[(b, i)][:],
-                                  in_=a_grouped[(b, i)][:].bitcast(BF16))
+        def quantise_supports(b):
+            a_codes[b] = work.tile([P, NS, NODES], U32, name="a_codes", bufs=3, align_bytes=64)
+            a_scales[b] = work.tile([P, NS, NODES], U8, name="a_scales", bufs=3, align_bytes=64)
+            nc.vector.quantize_mx(out=a_codes[b][:].rearrange("w i x -> w (i x)").bitcast(FP8X4),
+                                  scales=a_scales[b][:].rearrange("w i x -> w (i x)"),
+                                  in_=a_grouped[b][:].rearrange("w i x -> w (i x)").bitcast(BF16))
 
         def mx_product(b, i, u, codes, scales):
             ps = next_bank([P, 2, C_PAD], F32)
             for e in range(2):
-                first = 256 * e + P * u
-                nc.tensor.matmul_mx(out=ps[:, e, :], lhsT=a_codes[(b, i)][:, first:first + P].bitcast(FP8X4),
-                                    lhsT_scale=a_scales[(b, i)][:, first:first + P],
+                first = HALF * e + P * u
+                nc.tensor.matmul_mx(out=ps[:, e, :], lhsT=a_codes[b][:, i, first:first + P].bitcast(FP8X4),
+                                    lhsT_scale=a_scales[b][:, i, first:first + P],
                                     rhs=codes[:].bitcast(FP8X4), rhs_scale=scales[:], start=True, stop=True)
             return ps
 
@@ -182,13 +189,12 @@ def tile_dgggl_pa_t_kernel(tc, xg_gate, gate_w_z, gate_b_z, xt, state1, state2, 
         def quantise_t1(b):
             for i in range(NS):
                 first = 3 * C * i + C
-                nc.vector.tensor_copy(out=t1_grouped[(2 * b + i) % 4][:, 0:C, :],
-                                      in_=row[b][:, :, first:first + C].rearrange("p t c -> p c t"))
+                regroup(t1_grouped[(NS * b + i) % (2 * NS)][:, 0:C, :], row[b][:, :, first:first + C])
             for i in range(NS):
                 t1_codes[(b, i)] = work.tile([P, C_PAD], U32, name="t1_codes", bufs=4, align_bytes=64)
                 t1_scales[(b, i)] = work.tile([P, C_PAD], U8, name="t1_scales", bufs=4, align_bytes=64)
                 nc.vector.quantize_mx(out=t1_codes[(b, i)][:].bitcast(FP8X4), scales=t1_scales[(b, i)][:],
-                                      in_=t1_grouped[(2 * b + i) % 4][:].rearrange("p c t -> p (c t)"))
+                                      in_=t1_grouped[(NS * b + i) % (2 * NS)][:].rearrange("p c t -> p (c t)"))
 
         def second_product(b, i, u):
             ps = mx_product(b, i, u, t1_codes[(b, i)], t1_scales[(b, i)])
@@ -197,7 +203,7 @@ def tile_dgggl_pa_t_kernel(tc, xg_gate, gate_w_z, gate_b_z, xt, state1, state2, 
                                            in1=row[b][:, 2 * u:2 * u + 2, 0:C], op0=ALU.mult, op1=ALU.subtract)
 
         def store(b, u):
-            nc.sync.dma_start(out=work_order(out[b])[:, u], in_=row[b][:, 2 * u:2 * u + 2, :])
+            nc.sync.dma_start(out=out[b].rearrange("(u p e) f -> p u e f", u=2, e=2)[:, u], in_=row[b][:, 2 * u:2 * u + 2, :])
 
         def exists(b):
             return 0 <= b < B
@@ -217,9 +223,9 @@ def tile_dgggl_pa_t_kernel(tc, xg_gate, gate_w_z, gate_b_z, xt, state1, state2, 
                 load_states(2, B)
             if exists(n):
                 quantise_t1(n)
-            turn["gate_steps_left"] = GATE_STEPS if exists(n + 3) else 0
+            count["gate_steps_left"] = GATE_STEPS if exists(n + 3) else 0
             if n + 3 == 0:
-                for k in range(GATE_STEPS):
+                for step in range(GATE_STEPS):
                     gate_step(n + 3)
             if exists(n + 2):
                 candidate(n + 2)
@@ -228,12 +234,12 @@ def tile_dgggl_pa_t_kernel(tc, xg_gate, gate_w_z, gate_b_z, xt, state1, state2, 
                     for e in range(2):
                         transpose_supports(n + 2, i, e)
                         gate_step(n + 3)
-                    quantise_supports(n + 2, i)
+                quantise_supports(n + 2)
             if exists(n + 4):
-                for c in range(CHUNKS + 1):
-                    transpose_xg(n + 4, c)
+                for chunk in range(CHUNKS + 1):
+                    transpose_xg(n + 4, chunk)
                     gate_step(n + 3)
-            for k in range(GATE_STEPS):
+            for step in range(GATE_STEPS):
                 gate_step(n + 3)
             for u in range(2):
                 for i in range(NS):

@@ -211,7 +211,7 @@ def tile_dgggl_pa_t_kernel(tc, xg_gate, gate_w_z, gate_b_z, xt, state1, state2, 
         load_xg(0)
         load_weights()
         load_xg(1)
-        for n in range(-4, B):
+        for n in range(-4, B - 1):
             if exists(n + 4):
                 load_supports(n + 4)
             if exists(n + 6) and n + 6 >= 2:
@@ -221,8 +221,8 @@ def tile_dgggl_pa_t_kernel(tc, xg_gate, gate_w_z, gate_b_z, xt, state1, state2, 
                 group_xt(0)
             if n == -3:
                 load_states(2, B)
-            if exists(n):
-                quantise_t1(n)
+            if exists(n + 1):
+                quantise_t1(n + 1)
             count["gate_steps_left"] = GATE_STEPS if exists(n + 3) else 0
             if n + 3 == 0:
                 for step in range(GATE_STEPS):
@@ -243,9 +243,9 @@ def tile_dgggl_pa_t_kernel(tc, xg_gate, gate_w_z, gate_b_z, xt, state1, state2, 
                 gate_step(n + 3)
             for u in range(2):
                 for i in range(NS):
-                    if exists(n):
-                        second_product(n, i, u)
                     if exists(n + 1):
-                        first_product(n + 1, i, u)
-                if exists(n):
-                    store(n, u)
+                        second_product(n + 1, i, u)
+                    if exists(n + 2):
+                        first_product(n + 2, i, u)
+                if exists(n + 1):
+                    store(n + 1, u)

@@ -57,7 +57,7 @@ def tile_dgggl_pa_t_kernel(tc, xg_gate, gate_w_z, gate_b_z, xt, state1, state2, 
         for grouped in cand_grouped + t1_grouped:
             nc.vector.memset(grouped[:, C:C_PAD, :], 0.0)
 
-        xg_sb, a_sb, x_t, x_t_tail, gate_ps, z_t, z_ps, row = {}, {}, {}, {}, {}, {}, {}, {}
+        xg_sb, a_sb, a_sorted, x_t, x_t_tail, gate_ps, z_t, z_ps, row = {}, {}, {}, {}, {}, {}, {}, {}, {}
         a_grouped, a_codes, a_scales, cand_codes, cand_scales, t1_codes, t1_scales = {}, {}, {}, {}, {}, {}, {}
         count = {"banks_taken": 0, "gate_steps_left": 0}
 
@@ -89,10 +89,9 @@ def tile_dgggl_pa_t_kernel(tc, xg_gate, gate_w_z, gate_b_z, xt, state1, state2, 
 
         def load_states(b_from, b_to):
             pairs = ((xt, xt_sb[:, b_from:b_to]), (state1, st_sb[:, b_from:b_to, 0]), (state2, st_sb[:, b_from:b_to, 1]))
-            for u in range(2):
-                for src, dst in pairs:
-                    nc.sync.dma_start(out=dst[:, :, 2 * u:2 * u + 2, :].rearrange("p b e d -> p b (e d)"),
-                                      in_=src[b_from:b_to].rearrange("b (u p e) d -> u p b (e d)", u=2, e=2)[u])
+            for src, dst in pairs:
+                nc.sync.dma_start(out=dst.rearrange("p b j d -> p b (j d)"),
+                                  in_=src[b_from:b_to].rearrange("b (p j) d -> p b (j d)", j=SLOTS))
 
         def transpose_xg(b, chunk):
             if chunk == 0:
@@ -126,9 +125,7 @@ def tile_dgggl_pa_t_kernel(tc, xg_gate, gate_w_z, gate_b_z, xt, state1, state2, 
                 return
             nc.tensor.matmul(out=gate_ps[b][:], lhsT=w_tail[:], rhs=x_t_tail[b][:], start=False, stop=True)
             z_t[b] = work.tile([P, NODES], F32, name="z_t")
-            nc.scalar.activation(out=z_t[b][:].rearrange("g (e p q) -> g e p q", e=2, q=2),
-                                 in_=gate_ps[b][:].rearrange("g (q e p) -> g e p q", q=2, e=2),
-                                 func=ACT.Sigmoid, bias=bias_f[:, 0:1], scale=1.0)
+            nc.scalar.activation(out=z_t[b][:], in_=gate_ps[b][:], func=ACT.Sigmoid, bias=bias_f[:, 0:1], scale=1.0)
 
         def group_xt(b):
             regroup(cand_grouped[b % 2][:, 0:D, :], xt_sb[:, b])
@@ -136,8 +133,7 @@ def tile_dgggl_pa_t_kernel(tc, xg_gate, gate_w_z, gate_b_z, xt, state1, state2, 
         def candidate(b):
             z_ps[b] = next_bank([P, BANK], F32)
             for t in range(SLOTS):
-                first = HALF * (t % 2) + P * (t // 2)
-                nc.tensor.transpose(z_ps[b][:, P * t:P * t + P], z_t[b][:, first:first + P], ident_f[:])
+                nc.tensor.transpose(z_ps[b][:, P * t:P * t + P], z_t[b][:, P * t:P * t + P], ident_f[:])
             row[b] = rows.tile([P, SLOTS, F], F32, name="row")
             nc.vector.tensor_tensor(out=row[b][:, :, D:C].rearrange("p t (s d) -> p t s d", s=2),
                                     in0=z_ps[b][:].rearrange("p (t s d) -> p t s d", t=SLOTS, s=2),
@@ -153,17 +149,21 @@ def tile_dgggl_pa_t_kernel(tc, xg_gate, gate_w_z, gate_b_z, xt, state1, state2, 
             if b + 1 < B:
                 group_xt(b + 1)
 
-        def transpose_supports(b, i, e):
-            words = a_sb[b][:, i, :].bitcast(F32).rearrange("p (j w) -> p j w", j=SLOTS)
+        def sort_supports(b):
+            a_sorted[b] = work.tile([P, NS * SLOTS, 2, P], F32, name="a_sorted")
+            nc.vector.tensor_copy(out=a_sorted[b][:],
+                                  in_=a_sb[b][:].rearrange("p i x -> p (i x)").bitcast(F32).rearrange("p (r w v) -> p r v w", w=P, v=2))
+
+        def transpose_supports(b, i, h):
             ps = next_bank([P, BANK], F32)
-            for v in range(2):
-                for q in range(2):
-                    first = HALF * v + P * q
-                    nc.tensor.transpose(ps[:, first:first + P], words[:, 2 * q + e, P * v:P * v + P], ident_f[:])
-            if i == 0 and e == 0:
+            for k in range(2):
+                for v in range(2):
+                    first = HALF * k + P * v
+                    nc.tensor.transpose(ps[:, first:first + P], a_sorted[b][:, SLOTS * i + 2 * h + k, v, :], ident_f[:])
+            if i == 0 and h == 0:
                 a_grouped[b] = work.tile([P, NS, 2 * NODES], F32, name="a_grouped", align_bytes=64)
-            nc.scalar.copy(out=a_grouped[b][:, i, BANK * e:BANK * e + BANK].rearrange("w (p q v) -> w p q v", q=2, v=2),
-                           in_=ps[:].rearrange("w (v q p) -> w p q v", v=2, q=2))
+            nc.scalar.copy(out=a_grouped[b][:, i, BANK * h:BANK * h + BANK].rearrange("w (k p v) -> w k p v", k=2, v=2),
+                           in_=ps[:].rearrange("w (k v p) -> w k p v", k=2, v=2))
 
         def quantise_supports(b):
             a_codes[b] = work.tile([P, NS, NODES], U32, name="a_codes", bufs=3, align_bytes=64)
@@ -175,7 +175,7 @@ def tile_dgggl_pa_t_kernel(tc, xg_gate, gate_w_z, gate_b_z, xt, state1, state2, 
         def mx_product(b, i, u, codes, scales):
             ps = next_bank([P, 2, C_PAD], F32)
             for e in range(2):
-                first = HALF * e + P * u
+                first = P * (2 * u + e)
                 nc.tensor.matmul_mx(out=ps[:, e, :], lhsT=a_codes[b][:, i, first:first + P].bitcast(FP8X4),
                                     lhsT_scale=a_scales[b][:, i, first:first + P],
                                     rhs=codes[:].bitcast(FP8X4), rhs_scale=scales[:], start=True, stop=True)
@@ -203,7 +203,7 @@ def tile_dgggl_pa_t_kernel(tc, xg_gate, gate_w_z, gate_b_z, xt, state1, state2, 
                                            in1=row[b][:, 2 * u:2 * u + 2, 0:C], op0=ALU.mult, op1=ALU.subtract)
 
         def store(b, u):
-            nc.sync.dma_start(out=out[b].rearrange("(u p e) f -> p u e f", u=2, e=2)[:, u], in_=row[b][:, 2 * u:2 * u + 2, :])
+            nc.sync.dma_start(out=out[b].rearrange("(p u e) f -> p u e f", u=2, e=2)[:, u], in_=row[b][:, 2 * u:2 * u + 2, :])
 
         def exists(b):
             return 0 <= b < B
@@ -218,7 +218,6 @@ def tile_dgggl_pa_t_kernel(tc, xg_gate, gate_w_z, gate_b_z, xt, state1, state2, 
                 load_xg(n + 6)
             if n == -4:
                 load_states(0, 2)
-                group_xt(0)
             if n == -3:
                 load_states(2, B)
             if exists(n + 1):
@@ -235,17 +234,22 @@ def tile_dgggl_pa_t_kernel(tc, xg_gate, gate_w_z, gate_b_z, xt, state1, state2, 
                         transpose_supports(n + 2, i, e)
                         gate_step(n + 3)
                 quantise_supports(n + 2)
+            if exists(n + 3):
+                sort_supports(n + 3)
+            if n + 3 == 0:
+                group_xt(0)
             if exists(n + 4):
                 for chunk in range(CHUNKS + 1):
                     transpose_xg(n + 4, chunk)
                     gate_step(n + 3)
             for step in range(GATE_STEPS):
                 gate_step(n + 3)
-            for u in range(2):
-                for i in range(NS):
-                    if exists(n + 1):
+            if exists(n + 1):
+                for u in range(2):
+                    for i in range(NS):
                         second_product(n + 1, i, u)
-                    if exists(n + 2):
-                        first_product(n + 2, i, u)
-                if exists(n + 1):
                     store(n + 1, u)
+            if exists(n + 2):
+                for u in range(2):
+                    for i in range(NS):
+                        first_product(n + 2, i, u)

@@ -29,6 +29,8 @@ BANK = 512
 RUN = 4
 TURN_BANKS = 7
 
+UNSORTED = 2
+WARM_UP = 24
 FLOPS = 2 * B * NODES * F * G + 2 * NS * 2 * B * NODES * NODES * C
 
 
@@ -156,10 +158,14 @@ def tile_dgggl_pa_t_kernel(tc, xg_gate, gate_w_z, gate_b_z, xt, state1, state2, 
 
         def transpose_supports(b, i, h):
             ps = next_bank([P, BANK], F32)
+            words = a_sb[b][:, i, :].bitcast(F32).rearrange("p (j w v) -> p j v w", j=SLOTS, v=2)
             for k in range(2):
                 for v in range(2):
                     first = HALF * k + P * v
-                    nc.tensor.transpose(ps[:, first:first + P], a_sorted[b][:, SLOTS * i + 2 * h + k, v, :], ident_f[:])
+                    if b >= B - UNSORTED:
+                        nc.tensor.transpose(ps[:, first:first + P], words[:, 2 * h + k, v, :], ident_f[:])
+                    else:
+                        nc.tensor.transpose(ps[:, first:first + P], a_sorted[b][:, SLOTS * i + 2 * h + k, v, :], ident_f[:])
             if i == 0 and h == 0:
                 a_grouped[b] = work.tile([P, NS, 2 * NODES], F32, name="a_grouped", align_bytes=64)
             nc.scalar.copy(out=a_grouped[b][:, i, BANK * h:BANK * h + BANK].rearrange("w (k p v) -> w k p v", k=2, v=2),
@@ -209,6 +215,9 @@ def tile_dgggl_pa_t_kernel(tc, xg_gate, gate_w_z, gate_b_z, xt, state1, state2, 
             return 0 <= b < B
 
         load_xg(0)
+        warm_ps = psum.tile([P, P], F32, name="gate_ps", tag="gate_ps")
+        for k in range(WARM_UP):
+            nc.tensor.matmul(out=warm_ps[:], lhsT=ident_b[:], rhs=ident_b[:], start=True, stop=True)
         load_weights()
         load_xg(1)
         for n in range(-4, B - 1):
@@ -234,7 +243,7 @@ def tile_dgggl_pa_t_kernel(tc, xg_gate, gate_w_z, gate_b_z, xt, state1, state2, 
                         transpose_supports(n + 2, i, e)
                         gate_step(n + 3)
                 quantise_supports(n + 2)
-            if exists(n + 3):
+            if exists(n + 3) and n + 3 < B - UNSORTED:
                 sort_supports(n + 3)
             if n + 3 == 0:
                 group_xt(0)

@@ -112,8 +112,8 @@ def tile_dgggl_pa_t_kernel(tc, xg_gate, gate_w_z, gate_b_z, xt, state1, state2, 
                     nc.tensor.transpose(ps[:, P * j:P * j + P], xg_sb[b][:, F * j + 2 * P * CHUNKS:F * j + F], ident_b[:])
                 nc.scalar.copy(out=x_t_tail[b][:], in_=ps[:])
 
-        def gate_step(b):
-            if count["gate_steps_left"] == 0:
+        def gate_step(b, keep=0):
+            if count["gate_steps_left"] <= keep:
                 return
             step = GATE_STEPS - count["gate_steps_left"]
             count["gate_steps_left"] -= 1
@@ -142,12 +142,14 @@ def tile_dgggl_pa_t_kernel(tc, xg_gate, gate_w_z, gate_b_z, xt, state1, state2, 
                                     in1=st_sb[:, b].rearrange("p s t d -> p t s d"), op=ALU.mult)
             grouped = cand_grouped[b % 2]
             regroup(grouped[:, D:C, :], row[b][:, :, D:C])
-            nc.vector.tensor_copy(out=row[b][:, :, 0:D], in_=xt_sb[:, b])
+            if b < B - UNSORTED:
+                nc.vector.tensor_copy(out=row[b][:, :, 0:D], in_=xt_sb[:, b])
             cand_codes[b] = work.tile([P, C_PAD], U32, name="cand_codes", align_bytes=64)
             cand_scales[b] = work.tile([P, C_PAD], U8, name="cand_scales", align_bytes=64)
             nc.vector.quantize_mx(out=cand_codes[b][:].bitcast(FP8X4), scales=cand_scales[b][:],
                                   in_=grouped[:].rearrange("p c t -> p (c t)"))
-            nc.vector.tensor_copy(out=row[b][:, :, 3 * C:4 * C], in_=row[b][:, :, 0:C])
+            if b < B - UNSORTED:
+                nc.vector.tensor_copy(out=row[b][:, :, 3 * C:4 * C], in_=row[b][:, :, 0:C])
             if b + 1 < B:
                 group_xt(b + 1)
 
@@ -235,13 +237,17 @@ def tile_dgggl_pa_t_kernel(tc, xg_gate, gate_w_z, gate_b_z, xt, state1, state2, 
             if n + 3 == 0:
                 for step in range(GATE_STEPS):
                     gate_step(n + 3)
+            gate_step(n + 3)
             if exists(n + 2):
                 candidate(n + 2)
-                gate_step(n + 3)
+                gate_step(n + 3, keep=1)
                 for i in range(NS):
                     for e in range(2):
                         transpose_supports(n + 2, i, e)
-                        gate_step(n + 3)
+                        gate_step(n + 3, keep=1)
+                if n + 2 >= B - UNSORTED:
+                    nc.scalar.copy(out=row[n + 2][:, :, 0:D], in_=xt_sb[:, n + 2])
+                    nc.scalar.copy(out=row[n + 2][:, :, 3 * C:4 * C], in_=row[n + 2][:, :, 0:C])
                 quantise_supports(n + 2)
             if exists(n + 3) and n + 3 < B - UNSORTED:
                 sort_supports(n + 3)
@@ -250,7 +256,7 @@ def tile_dgggl_pa_t_kernel(tc, xg_gate, gate_w_z, gate_b_z, xt, state1, state2, 
             if exists(n + 4):
                 for chunk in range(CHUNKS + 1):
                     transpose_xg(n + 4, chunk)
-                    gate_step(n + 3)
+                    gate_step(n + 3, keep=1)
             for step in range(GATE_STEPS):
                 gate_step(n + 3)
             if exists(n + 1):

@@ -31,6 +31,7 @@ TURN_BANKS = 7
 
 UNSORTED = 2
 WARM_UP = 24
+HALVED = 2
 FLOPS = 2 * B * NODES * F * G + 2 * NS * 2 * B * NODES * NODES * C
 
 
@@ -210,8 +211,8 @@ def tile_dgggl_pa_t_kernel(tc, xg_gate, gate_w_z, gate_b_z, xt, state1, state2, 
             nc.vector.scalar_tensor_tensor(out=row[b][:, 2 * u:2 * u + 2, first:first + C], in0=ps[:, :, 0:C], scalar=2.0,
                                            in1=row[b][:, 2 * u:2 * u + 2, 0:C], op0=ALU.mult, op1=ALU.subtract)
 
-        def store(b, u):
-            nc.sync.dma_start(out=out[b].rearrange("(p u e) f -> p u e f", u=2, e=2)[:, u], in_=row[b][:, 2 * u:2 * u + 2, :])
+        def store(b, slots):
+            nc.sync.dma_start(out=out[b].rearrange("(p j) f -> p j f", j=SLOTS)[:, slots, :], in_=row[b][:, slots, :])
 
         def exists(b):
             return 0 <= b < B
@@ -263,7 +264,10 @@ def tile_dgggl_pa_t_kernel(tc, xg_gate, gate_w_z, gate_b_z, xt, state1, state2, 
                 for u in range(2):
                     for i in range(NS):
                         second_product(n + 1, i, u)
-                    store(n + 1, u)
+                    if n + 1 >= B - HALVED:
+                        store(n + 1, slice(2 * u, 2 * u + 2))
+                if n + 1 < B - HALVED:
+                    store(n + 1, slice(0, SLOTS))
             if exists(n + 2):
                 for u in range(2):
                     for i in range(NS):

@@ -45,10 +45,13 @@ def tile_dgggl_pa_t_kernel(tc, xg_gate, gate_w_z, gate_b_z, xt, state1, state2, 
         psum = ctx.enter_context(tc.psum_pool(name="psum", bufs=1))
         ctx.enter_context(tc.manual_schedule())
 
-        ident_f = const.tile([P, P], F32, name="ident_f")
-        make_identity(nc, ident_f[:])
+        one_column = const.tile([P, 1], F32, name="one_column")
+        nc.vector.memset(one_column[:], 0.0)
+        nc.scalar.activation(out=one_column[:], in_=one_column[:], func=ACT.Sigmoid)
         ident_b = const.tile([P, P], BF16, name="ident_b")
         make_identity(nc, ident_b[:])
+        ident_f = const.tile([P, P], F32, name="ident_f")
+        make_identity(nc, ident_f[:])
         w_sb = const.tile([P, CHUNKS, 2, G], BF16, name="w_sb")
         w_tail = const.tile([P, G], BF16, name="w_tail")
         bias_b = const.tile([P, 1], BF16, name="bias_b")

from contextlib import ExitStack

import concourse.mybir as mybir
from concourse.masks import make_identity

F32 = mybir.dt.float32
BF16 = mybir.dt.bfloat16
U32 = mybir.dt.uint32
U8 = mybir.dt.uint8
FP8X4 = mybir.dt.float8_e4m3fn_x4
ALU = mybir.AluOpType
ACT = mybir.ActivationFunctionType

P = 128
B = 8
NODES = 512
SLOTS = NODES // P
HALF = NODES // 2
F = 1152
D = 64
G = 2 * D
C = 3 * D
C_PAD = 256
NS = 2
WORDS = F // 2
CHUNKS = 4
GATE_STEPS = 2 * CHUNKS + 1
BANK = 512
RUN = 4
TURN_BANKS = 7

UNSORTED = 2
WARM_UP = 24
HALVED = 2
FLOPS = 2 * B * NODES * F * G + 2 * NS * 2 * B * NODES * NODES * C


def tile_dgggl_pa_t_kernel(tc, xg_gate, gate_w_z, gate_b_z, xt, state1, state2, supports, out):
    nc = tc.nc
    with ExitStack() as ctx:
        const = ctx.enter_context(tc.tile_pool(name="const", bufs=1))
        loads = ctx.enter_context(tc.tile_pool(name="loads", bufs=3))
        work = ctx.enter_context(tc.tile_pool(name="work", bufs=2))
        rows = ctx.enter_context(tc.tile_pool(name="rows", bufs=4))
        psum = ctx.enter_context(tc.psum_pool(name="psum", bufs=1))
        ctx.enter_context(tc.manual_schedule())

        one_column = const.tile([P, 1], F32, name="one_column")
        nc.vector.memset(one_column[:], 0.0)
        nc.scalar.activation(out=one_column[:], in_=one_column[:], func=ACT.Sigmoid)
        ident_b = const.tile([P, P], BF16, name="ident_b")
        make_identity(nc, ident_b[:])
        ident_f = const.tile([P, P], F32, name="ident_f")
        make_identity(nc, ident_f[:])
        w_sb = const.tile([P, CHUNKS, 2, G], BF16, name="w_sb")
        w_tail = const.tile([P, G], BF16, name="w_tail")
        bias_b = const.tile([P, 1], BF16, name="bias_b")
        bias_f = const.tile([P, 1], F32, name="bias_f")
        xt_sb = const.tile([P, B, SLOTS, D], BF16, name="xt_sb")
        st_sb = const.tile([P, B, 2, SLOTS, D], BF16, name="st_sb")
        cand_grouped = [const.tile([P, C_PAD, SLOTS], BF16, name="cand_grouped%d" % k, align_bytes=64) for k in range(2)]
        t1_grouped = [const.tile([P, C_PAD, SLOTS], BF16, name="t1_grouped%d" % k, align_bytes=64) for k in range(2 * NS)]
        for grouped in cand_grouped + t1_grouped:
            nc.vector.memset(grouped[:, C:C_PAD, :], 0.0)

        xg_sb, a_sb, a_sorted, x_t, x_t_tail, gate_ps, z_t, z_ps, row = {}, {}, {}, {}, {}, {}, {}, {}, {}
        a_grouped, a_codes, a_scales, cand_codes, cand_scales, t1_codes, t1_scales = {}, {}, {}, {}, {}, {}, {}
        count = {"banks_taken": 0, "gate_steps_left": 0}

        def next_bank(shape, dtype):
            k = count["banks_taken"] % TURN_BANKS
            count["banks_taken"] += 1
            return psum.tile(shape, dtype, name="turn%d" % k, tag="turn%d" % k)

        def regroup(grouped_columns, slot_columns):
            nc.vector.tensor_copy(out=grouped_columns.rearrange("p (c r) t -> p c t r", r=RUN),
                                  in_=slot_columns.rearrange("p t (c r) -> p c t r", r=RUN))

        def load_xg(b):
            xg_sb[b] = loads.tile([P, SLOTS * F], BF16, name="xg_sb")
            nc.sync.dma_start(out=xg_sb[b][:], in_=xg_gate[b].rearrange("(p j) f -> p (j f)", j=SLOTS))

        def load_supports(b):
            a_sb[b] = loads.tile([P, NS, SLOTS * NODES], BF16, name="a_sb")
            for i in range(NS):
                nc.sync.dma_start(out=a_sb[b][:, i, :], in_=supports[i, b].rearrange("(p j) m -> p (j m)", j=SLOTS))

        def load_weights():
            nc.sync.dma_start(out=w_sb[:].rearrange("w h r g -> w h (r g)"),
                              in_=gate_w_z[0:2 * P * CHUNKS, :].rearrange("(h w r) g -> w h (r g)", h=CHUNKS, r=2))
            nc.sync.dma_start(out=w_tail[:], in_=gate_w_z[2 * P * CHUNKS:F, :])
            with nc.allow_non_contiguous_dma(reason="one bias value to a partition"):
                nc.sync.dma_start(out=bias_b[:], in_=gate_b_z.rearrange("(g o) -> g o", o=1))
            nc.vector.tensor_copy(out=bias_f[:], in_=bias_b[:])

        def load_states(b_from, b_to):
            pairs = ((xt, xt_sb[:, b_from:b_to]), (state1, st_sb[:, b_from:b_to, 0]), (state2, st_sb[:, b_from:b_to, 1]))
            for src, dst in pairs:
                nc.sync.dma_start(out=dst.rearrange("p b j d -> p b (j d)"),
                                  in_=src[b_from:b_to].rearrange("b (p j) d -> p b (j d)", j=SLOTS))

        def transpose_xg(b, chunk):
            if chunk == 0:
                x_t[b] = work.tile([P, CHUNKS * NODES], F32, name="x_t")
                x_t_tail[b] = work.tile([P, NODES], BF16, name="x_t_tail")
            if chunk < CHUNKS:
                words = xg_sb[b][:].bitcast(F32)
                ps = next_bank([P, BANK], F32)
                for j in range(SLOTS):
                    first = WORDS * j + P * chunk
                    nc.tensor.transpose(ps[:, P * j:P * j + P], words[:, first:first + P], ident_f[:])
                nc.scalar.copy(out=x_t[b][:, NODES * chunk:NODES * chunk + NODES], in_=ps[:])
            else:
                ps = next_bank([P, NODES], BF16)
                for j in range(SLOTS):
                    nc.tensor.transpose(ps[:, P * j:P * j + P], xg_sb[b][:, F * j + 2 * P * CHUNKS:F * j + F], ident_b[:])
                nc.scalar.copy(out=x_t_tail[b][:], in_=ps[:])

        def gate_step(b, keep=0):
            if count["gate_steps_left"] <= keep:
                return
            step = GATE_STEPS - count["gate_steps_left"]
            count["gate_steps_left"] -= 1
            if step == 0:
                gate_ps[b] = psum.tile([P, NODES], F32, name="gate_ps", tag="gate_ps")
            if step < 2 * CHUNKS:
                chunk, r = step // 2, step % 2
                halves = x_t[b][:].bitcast(BF16).rearrange("w (h x r) -> w h x r", h=CHUNKS, r=2)
                nc.tensor.matmul(out=gate_ps[b][:], lhsT=w_sb[:, chunk, r, :], rhs=halves[:, chunk, :, r],
                                 start=(step == 0), stop=False)
                return
            nc.tensor.matmul(out=gate_ps[b][:], lhsT=w_tail[:], rhs=x_t_tail[b][:], start=False, stop=True)
            z_t[b] = work.tile([P, NODES], F32, name="z_t")
            nc.scalar.activation(out=z_t[b][:], in_=gate_ps[b][:], func=ACT.Sigmoid, bias=bias_f[:, 0:1], scale=1.0)

        def group_xt(b):
            regroup(cand_grouped[b % 2][:, 0:D, :], xt_sb[:, b])

        def candidate(b):
            z_ps[b] = next_bank([P, BANK], F32)
            for t in range(SLOTS):
                nc.tensor.transpose(z_ps[b][:, P * t:P * t + P], z_t[b][:, P * t:P * t + P], ident_f[:])
            row[b] = rows.tile([P, SLOTS, F], F32, name="row")
            nc.vector.tensor_tensor(out=row[b][:, :, D:C].rearrange("p t (s d) -> p t s d", s=2),
                                    in0=z_ps[b][:].rearrange("p (t s d) -> p t s d", t=SLOTS, s=2),
                                    in1=st_sb[:, b].rearrange("p s t d -> p t s d"), op=ALU.mult)
            grouped = cand_grouped[b % 2]
            regroup(grouped[:, D:C, :], row[b][:, :, D:C])
            if b < B - UNSORTED:
                nc.vector.tensor_copy(out=row[b][:, :, 0:D], in_=xt_sb[:, b])
            cand_codes[b] = work.tile([P, C_PAD], U32, name="cand_codes", align_bytes=64)
            cand_scales[b] = work.tile([P, C_PAD], U8, name="cand_scales", align_bytes=64)
            nc.vector.quantize_mx(out=cand_codes[b][:].bitcast(FP8X4), scales=cand_scales[b][:],
                                  in_=grouped[:].rearrange("p c t -> p (c t)"))
            if b < B - UNSORTED:
                nc.vector.tensor_copy(out=row[b][:, :, 3 * C:4 * C], in_=row[b][:, :, 0:C])
            if b + 1 < B:
                group_xt(b + 1)

        def sort_supports(b):
            a_sorted[b] = work.tile([P, NS * SLOTS, 2, P], F32, name="a_sorted")
            nc.vector.tensor_copy(out=a_sorted[b][:],
                                  in_=a_sb[b][:].rearrange("p i x -> p (i x)").bitcast(F32).rearrange("p (r w v) -> p r v w", w=P, v=2))

        def transpose_supports(b, i, h):
            ps = next_bank([P, BANK], F32)
            words = a_sb[b][:, i, :].bitcast(F32).rearrange("p (j w v) -> p j v w", j=SLOTS, v=2)
            for k in range(2):
                for v in range(2):
                    first = HALF * k + P * v
                    if b >= B - UNSORTED:
                        nc.tensor.transpose(ps[:, first:first + P], words[:, 2 * h + k, v, :], ident_f[:])
                    else:
                        nc.tensor.transpose(ps[:, first:first + P], a_sorted[b][:, SLOTS * i + 2 * h + k, v, :], ident_f[:])
            if i == 0 and h == 0:
                a_grouped[b] = work.tile([P, NS, 2 * NODES], F32, name="a_grouped", align_bytes=64)
            nc.scalar.copy(out=a_grouped[b][:, i, BANK * h:BANK * h + BANK].rearrange("w (k p v) -> w k p v", k=2, v=2),
                           in_=ps[:].rearrange("w (k v p) -> w k p v", k=2, v=2))

        def quantise_supports(b):
            a_codes[b] = work.tile([P, NS, NODES], U32, name="a_codes", bufs=3, align_bytes=64)
            a_scales[b] = work.tile([P, NS, NODES], U8, name="a_scales", bufs=3, align_bytes=64)
            nc.vector.quantize_mx(out=a_codes[b][:].rearrange("w i x -> w (i x)").bitcast(FP8X4),
                                  scales=a_scales[b][:].rearrange("w i x -> w (i x)"),
                                  in_=a_grouped[b][:].rearrange("w i x -> w (i x)").bitcast(BF16))

        def mx_product(b, i, u, codes, scales):
            ps = next_bank([P, 2, C_PAD], F32)
            for e in range(2):
                first = P * (2 * u + e)
                nc.tensor.matmul_mx(out=ps[:, e, :], lhsT=a_codes[b][:, i, first:first + P].bitcast(FP8X4),
                                    lhsT_scale=a_scales[b][:, i, first:first + P],
                                    rhs=codes[:].bitcast(FP8X4), rhs_scale=scales[:], start=True, stop=True)
            return ps

        def first_product(b, i, u):
            ps = mx_product(b, i, u, cand_codes[b], cand_scales[b])
            first = 3 * C * i + C
            nc.scalar.copy(out=row[b][:, 2 * u:2 * u + 2, first:first + C], in_=ps[:, :, 0:C])

        def quantise_t1(b):
            for i in range(NS):
                first = 3 * C * i + C
                regroup(t1_grouped[(NS * b + i) % (2 * NS)][:, 0:C, :], row[b][:, :, first:first + C])
            for i in range(NS):
                t1_codes[(b, i)] = work.tile([P, C_PAD], U32, name="t1_codes", bufs=4, align_bytes=64)
                t1_scales[(b, i)] = work.tile([P, C_PAD], U8, name="t1_scales", bufs=4, align_bytes=64)
                nc.vector.quantize_mx(out=t1_codes[(b, i)][:].bitcast(FP8X4), scales=t1_scales[(b, i)][:],
                                      in_=t1_grouped[(NS * b + i) % (2 * NS)][:].rearrange("p c t -> p (c t)"))

        def second_product(b, i, u):
            ps = mx_product(b, i, u, t1_codes[(b, i)], t1_scales[(b, i)])
            first = 3 * C * i + 2 * C
            nc.vector.scalar_tensor_tensor(out=row[b][:, 2 * u:2 * u + 2, first:first + C], in0=ps[:, :, 0:C], scalar=2.0,
                                           in1=row[b][:, 2 * u:2 * u + 2, 0:C], op0=ALU.mult, op1=ALU.subtract)

        def store(b, slots):
            nc.sync.dma_start(out=out[b].rearrange("(p j) f -> p j f", j=SLOTS)[:, slots, :], in_=row[b][:, slots, :])

        def exists(b):
            return 0 <= b < B

        load_xg(0)
        warm_ps = psum.tile([P, P], F32, name="gate_ps", tag="gate_ps")
        for k in range(WARM_UP):
            nc.tensor.matmul(out=warm_ps[:], lhsT=ident_b[:], rhs=ident_b[:], start=True, stop=True)
        load_weights()
        load_xg(1)
        for n in range(-4, B - 1):
            if exists(n + 4):
                load_supports(n + 4)
            if exists(n + 6) and n + 6 >= 2:
                load_xg(n + 6)
            if n == -4:
                load_states(0, 2)
            if n == -3:
                load_states(2, B)
            if exists(n + 1):
                quantise_t1(n + 1)
            count["gate_steps_left"] = GATE_STEPS if exists(n + 3) else 0
            if n + 3 == 0:
                for step in range(GATE_STEPS):
                    gate_step(n + 3)
            gate_step(n + 3)
            if exists(n + 2):
                candidate(n + 2)
                gate_step(n + 3, keep=1)
                for i in range(NS):
                    for e in range(2):
                        transpose_supports(n + 2, i, e)
                        gate_step(n + 3, keep=1)
                if n + 2 >= B - UNSORTED:
                    nc.scalar.copy(out=row[n + 2][:, :, 0:D], in_=xt_sb[:, n + 2])
                    nc.scalar.copy(out=row[n + 2][:, :, 3 * C:4 * C], in_=row[n + 2][:, :, 0:C])
                quantise_supports(n + 2)
            if exists(n + 3) and n + 3 < B - UNSORTED:
                sort_supports(n + 3)
            if n + 3 == 0:
                group_xt(0)
            if exists(n + 4):
                for chunk in range(CHUNKS + 1):
                    transpose_xg(n + 4, chunk)
                    gate_step(n + 3, keep=1)
            for step in range(GATE_STEPS):
                gate_step(n + 3)
            if exists(n + 1):
                for u in range(2):
                    for i in range(NS):
                        second_product(n + 1, i, u)
                    if n + 1 >= B - HALVED:
                        store(n + 1, slice(2 * u, 2 * u + 2))
                if n + 1 < B - HALVED:
                    store(n + 1, slice(0, SLOTS))
            if exists(n + 2):
                for u in range(2):
                    for i in range(NS):
                        first_product(n + 2, i, u)
